import numpy as np
import ml_dtypes


def mxq(x, axis, fmt="e4m3"):
    dtype, down = {"e4m3": (ml_dtypes.float8_e4m3fn, 7), "e5m2": (ml_dtypes.float8_e5m2, 14)}[fmt]
    v = np.moveaxis(np.asarray(x, np.float32).astype(ml_dtypes.bfloat16).astype(np.float64), axis, -1)
    blocks = v.reshape(v.shape[:-1] + (-1, 32))
    amax = np.abs(blocks).max(-1, keepdims=True)
    byte = np.maximum(np.where(amax > 0, np.frexp(amax)[1] - 1 + 127, 0) - down, 1)
    scale = np.exp2(byte - 127.0)
    codes = (blocks / scale).astype(np.float32).astype(dtype).astype(np.float64)
    return np.moveaxis((codes * scale).reshape(v.shape), -1, axis)


WIDE = False


def mx_kscale(k):
    if not WIDE:
        return np.ones(k)
    levels = np.array([10, -10, 5, -5, 0])
    a = np.random.permutation(np.resize(levels, k // 512 * 4)).reshape(k // 512, 4)
    idx = np.arange(k)
    return np.exp2(a[idx // 512, idx % 128 // 32])


BF16 = ml_dtypes.bfloat16


def bf(x):
    return np.asarray(x, np.float32).astype(BF16)


def f64(x):
    return np.asarray(x).astype(np.float64)


B, H, S, D, QB = 4, 8, 512, 128, 512
EPS = 1e-6
A = (4.0 * EPS / S) ** 0.25


def setup_inputs():
    t = np.exp2(np.round(np.log2(mx_kscale(S)) / 2))
    c = 4.0 ** np.round(np.log2(np.mean(t * t)) / 2)
    return {"q": bf(np.random.standard_normal((B, H, S, D)) * A / np.sqrt(c)),
            "k": bf(np.random.standard_normal((B, H, S, D)) * A * t[:, None]),
            "v": bf(np.random.standard_normal((B, H, S, D)) * 0.2 * np.sqrt(S) * c / (t * t)[:, None])}


def reference(q, k, v):
    q, k = f64(q), f64(k)
    scale = D ** (-0.5)
    vq = mxq(f64(v), 2, "e4m3")
    out = []
    for lo in range(0, S, QB):
        hi = lo + QB
        s = q[:, :, lo:hi] @ k[:, :, :hi].transpose(0, 1, 3, 2) * scale
        s2 = s * s
        causal = np.arange(hi)[None, :] <= np.arange(lo, hi)[:, None]
        s2 = np.where(causal, s2, 0.0)
        z = s2.sum(-1)
        o = mxq(s2, 3, "e4m3") @ vq[:, :, :hi]
        out.append(o / (z[..., None] + EPS))
    return np.concatenate(out, axis=2)

@@ -1,0 +1,234 @@
+from contextlib import ExitStack
+
+import concourse.mybir as mybir
+from concourse.masks import make_identity
+
+F32 = mybir.dt.float32
+BF16 = mybir.dt.bfloat16
+U32 = mybir.dt.uint32
+U8 = mybir.dt.uint8
+FP8X4 = mybir.dt.float8_e4m3fn_x4
+ACT = mybir.ActivationFunctionType
+ALU = mybir.AluOpType
+
+B, H, S, D = 4, 8, 512, 128
+HEADS = B * H
+P = 128
+CHUNKS = S // P
+PACK = 4
+QUARTER = P // PACK
+GROUP = 4
+SLOTS = 4
+EPS = 1e-6
+SCALE = D ** -0.5
+
+FLOPS = 2 * (2 * HEADS * S * S * D)
+
+
+def tile_modelnew_t_kernel(tc, q, k, v, out):
+    nc = tc.nc
+    q_rows = q.rearrange("b h (c m) d -> m (b h c) d", m=P)
+    k_rows = k.rearrange("b h (p j) d -> p (b h) (j d)", j=PACK)
+    v_rows = v.rearrange("b h (p j) d -> p (b h) (j d)", j=PACK)
+    out_rows = out.rearrange("b h (c m) d -> m (b h) c d", m=P)
+
+    with ExitStack() as ctx:
+        const = ctx.enter_context(tc.tile_pool(name="const", bufs=1))
+        loads = ctx.enter_context(tc.tile_pool(name="loads", bufs=1))
+        keep = ctx.enter_context(tc.tile_pool(name="keep", bufs=1))
+        work = ctx.enter_context(tc.tile_pool(name="work", bufs=3))
+        psum = ctx.enter_context(tc.psum_pool(name="psum", bufs=1))
+
+        ident_bf = const.tile([P, P], BF16)
+        make_identity(nc, ident_bf[:])
+        ident_f32 = const.tile([P, P], F32)
+        make_identity(nc, ident_f32[:])
+        causal = const.tile([P, P], F32)
+        nc.gpsimd.memset(causal[:], 1.0)
+        nc.gpsimd.affine_select(
+            out=causal[:],
+            in_=causal[:],
+            compare_op=ALU.is_ge,
+            fill=0.0,
+            base=0,
+            pattern=[[-1, P]],
+            channel_multiplier=1,
+        )
+        causal_jw = const.tile([P, P], F32)
+        nc.vector.tensor_copy(
+            out=causal_jw[:].rearrange("m (j w) -> m j w", j=PACK),
+            in_=causal[:].rearrange("m (w j) -> m j w", j=PACK),
+        )
+
+        q_sb, k_sb, v_sb = [], [], []
+        for g in range(HEADS // GROUP):
+            heads = slice(g * GROUP, (g + 1) * GROUP)
+            q_g = loads.tile([P, GROUP * CHUNKS, D], BF16, name="q_g%d" % g)
+            nc.sync.dma_start(out=q_g[:], in_=q_rows[:, g * GROUP * CHUNKS : (g + 1) * GROUP * CHUNKS, :])
+            k_g = loads.tile([P, GROUP, PACK * D], BF16, name="k_g%d" % g)
+            nc.sync.dma_start(out=k_g[:], in_=k_rows[:, heads, :])
+            v_g = loads.tile([P, GROUP, PACK * D], BF16, name="v_g%d" % g)
+            nc.sync.dma_start(out=v_g[:], in_=v_rows[:, heads, :])
+            q_sb.append(q_g)
+            k_sb.append(k_g)
+            v_sb.append(v_g)
+
+        v_codes = keep.tile([P, HEADS * D], U32, align_bytes=64)
+        v_scales = keep.tile([P, HEADS * D], U8, align_bytes=64)
+        squares, row_sums = [], []
+        for slot in range(SLOTS):
+            s2 = keep.tile([P, CHUNKS * S], BF16, name="s2_%d" % slot)
+            nc.vector.memset(s2[:], 0.0)
+            z = keep.tile([P, 2 * CHUNKS], F32, name="z_%d" % slot)
+            nc.vector.memset(z[:], 0.0)
+            squares.append(s2)
+            row_sums.append(z)
+
+        transposed = {}
+        quantised = {}
+
+        def quantise_v(g):
+            grouped_v = work.tile([P, GROUP, D, PACK], BF16, align_bytes=64, tag="grouped_v", bufs=2)
+            nc.vector.tensor_copy(
+                out=grouped_v[:],
+                in_=v_sb[g][:].rearrange("p g (j d) -> p g d j", j=PACK),
+            )
+            cols = slice(g * GROUP * D, (g + 1) * GROUP * D)
+            nc.vector.quantize_mx(
+                out=v_codes[:, cols].bitcast(FP8X4),
+                scales=v_scales[:, cols],
+                in_=grouped_v[:].rearrange("p g d j -> p (g d j)"),
+            )
+
+        def transpose_q_k(h):
+            g, i = divmod(h, GROUP)
+            qk_ps = psum.tile([P, 2 * S], BF16, tag="qk_ps")
+            for c in range(CHUNKS):
+                nc.tensor.transpose(qk_ps[:, c * P : (c + 1) * P], q_sb[g][:, i * CHUNKS + c, :], ident_bf[:])
+            for j in range(PACK):
+                nc.tensor.transpose(
+                    qk_ps[:, S + j * P : S + (j + 1) * P], k_sb[g][:, i, j * D : (j + 1) * D], ident_bf[:]
+                )
+            qk_t = work.tile([P, 2 * S], BF16, tag="qk_t")
+            nc.scalar.copy(out=qk_t[:], in_=qk_ps[:])
+            transposed[h] = qk_t
+
+        def scores_and_squares(h):
+            qk_t = transposed[h]
+            k_t = qk_t[:, S : 2 * S].rearrange("d (j p) -> d j p", j=PACK)
+            s2 = squares[h % SLOTS][:].rearrange("m (c u x) -> m c u x", c=CHUNKS, u=2)
+            z = row_sums[h % SLOTS]
+            diag_ps = psum.tile([P, S], F32, tag="diag_ps")
+            past_a = psum.tile([P, S], F32, tag="past_a")
+            past_b = psum.tile([P, 2 * P], F32, tag="past_b")
+            past = {1: past_a[:, 0:P], 3: past_a[:, P : 4 * P], 2: past_b[:, 0 : 2 * P]}
+            for c in range(CHUNKS):
+                q_t = qk_t[:, c * P : (c + 1) * P]
+                nc.tensor.matmul(
+                    out=diag_ps[:, c * P : (c + 1) * P].rearrange("m (j w) -> m j w", j=PACK),
+                    lhsT=q_t,
+                    rhs=k_t[:, :, c * QUARTER : (c + 1) * QUARTER],
+                    start=True,
+                    stop=True,
+                )
+                if c > 0:
+                    nc.tensor.matmul(
+                        out=past[c].rearrange("m (j w) -> m j w", j=PACK),
+                        lhsT=q_t,
+                        rhs=k_t[:, :, 0 : c * QUARTER],
+                        start=True,
+                        stop=True,
+                    )
+            masked = work.tile([P, S], F32, tag="masked")
+            nc.vector.tensor_tensor(
+                out=masked[:].rearrange("m (c x) -> m c x", c=CHUNKS),
+                in0=diag_ps[:].rearrange("m (c x) -> m c x", c=CHUNKS),
+                in1=causal_jw[:].unsqueeze(1).to_broadcast([P, CHUNKS, P]),
+                op=ALU.mult,
+            )
+            for c in range(CHUNKS):
+                seen = 2 * c * QUARTER
+                if c > 0:
+                    nc.scalar.activation(
+                        out=s2[:, c, :, 0:seen].rearrange("m u (w e) -> m u w e", e=2),
+                        in_=past[c].rearrange("m (u e w) -> m u w e", u=2, e=2),
+                        func=ACT.Square,
+                        scale=SCALE,
+                        accum_out=z[:, c : c + 1],
+                    )
+                nc.scalar.activation(
+                    out=s2[:, c, :, seen : seen + 2 * QUARTER].rearrange("m u (w e) -> m u w e", e=2),
+                    in_=masked[:, c * P : (c + 1) * P].rearrange("m (u e w) -> m u w e", u=2, e=2),
+                    func=ACT.Square,
+                    scale=SCALE,
+                    accum_out=z[:, CHUNKS + c : CHUNKS + c + 1],
+                )
+
+        def transpose_and_quantise(h):
+            words = squares[h % SLOTS][:].bitcast(F32)
+            grouped = work.tile([P, CHUNKS * P * PACK], BF16, align_bytes=64, tag="grouped")
+            grouped_words = grouped[:].bitcast(F32)
+            for half in range(2):
+                s2t_ps = psum.tile([P, S], F32, tag="s2t_ps", bufs=3)
+                for n in range(4):
+                    plane = 4 * half + n
+                    nc.tensor.transpose(
+                        s2t_ps[:, n * P : (n + 1) * P], words[:, plane * P : (plane + 1) * P], ident_f32[:]
+                    )
+                nc.vector.tensor_copy(
+                    out=grouped_words[:, half * S : (half + 1) * S].rearrange("p (c m u) -> p c m u", c=2, u=2),
+                    in_=s2t_ps[:].rearrange("p (c u m) -> p c m u", c=2, u=2),
+                )
+            codes = work.tile([P, S], U32, align_bytes=64, tag="codes")
+            scales = work.tile([P, S], U8, align_bytes=64, tag="scales")
+            nc.vector.quantize_mx(out=codes[:].bitcast(FP8X4), scales=scales[:], in_=grouped[:])
+            quantised[h] = (codes, scales)
+
+        def weighted_values(h):
+            codes, scales = quantised[h]
+            z = row_sums[h % SLOTS]
+            o_ps = psum.tile([P, S], F32, tag="o_ps")
+            v_cols = slice(h * D, (h + 1) * D)
+            for c in range(CHUNKS):
+                m_cols = slice(c * P, (c + 1) * P)
+                nc.tensor.matmul_mx(
+                    out=o_ps[:, m_cols],
+                    lhsT=codes[:, m_cols].bitcast(FP8X4),
+                    lhsT_scale=scales[:, m_cols],
+                    rhs=v_codes[:, v_cols].bitcast(FP8X4),
+                    rhs_scale=v_scales[:, v_cols],
+                    start=True,
+                    stop=True,
+                )
+            denom = work.tile([P, CHUNKS], F32, tag="denom")
+            nc.vector.scalar_tensor_tensor(
+                out=denom[:],
+                in0=z[:, 0:CHUNKS],
+                scalar=EPS,
+                in1=z[:, CHUNKS : 2 * CHUNKS],
+                op0=ALU.add,
+                op1=ALU.add,
+            )
+            inverse = work.tile([P, CHUNKS], F32, tag="inverse")
+            nc.vector.reciprocal(out=inverse[:], in_=denom[:])
+            o_sb = work.tile([P, CHUNKS, D], F32, tag="o_sb", bufs=4)
+            for c in range(CHUNKS):
+                nc.scalar.activation(
+                    out=o_sb[:, c, :],
+                    in_=o_ps[:, c * P : (c + 1) * P],
+                    func=ACT.Copy,
+                    scale=inverse[:, c : c + 1],
+                )
+            nc.sync.dma_start(out=out_rows[:, h, :, :], in_=o_sb[:])
+
+        for step in range(HEADS + 3):
+            if step < HEADS:
+                if step % GROUP == 0:
+                    quantise_v(step // GROUP)
+                transpose_q_k(step)
+            if 0 <= step - 1 < HEADS:
+                scores_and_squares(step - 1)
+            if 0 <= step - 2 < HEADS:
+                transpose_and_quantise(step - 2)
+            if 0 <= step - 3 < HEADS:
+                weighted_values(step - 3)

@@ -17,8 +17,8 @@ P = 128
 CHUNKS = S // P
 PACK = 4
 QUARTER = P // PACK
-GROUP = 4
-SLOTS = 4
+GROUP = 2
+SLOTS = 3
 EPS = 1e-6
 SCALE = D ** -0.5
 
@@ -84,20 +84,20 @@ def tile_modelnew_t_kernel(tc, q, k, v, out):
             squares.append(s2)
             row_sums.append(z)
 
-        transposed = {}
-        quantised = {}
+        live = {}
 
-        def quantise_v(g):
-            grouped_v = work.tile([P, GROUP, D, PACK], BF16, align_bytes=64, tag="grouped_v", bufs=2)
-            nc.vector.tensor_copy(
-                out=grouped_v[:],
-                in_=v_sb[g][:].rearrange("p g (j d) -> p g d j", j=PACK),
-            )
-            cols = slice(g * GROUP * D, (g + 1) * GROUP * D)
+        def quantise_v(h):
+            g, i = divmod(h, GROUP)
+            grouped_v = work.tile([P, D, PACK], BF16, align_bytes=64, tag="grouped_v")
+            nc.vector.tensor_copy(out=grouped_v[:], in_=v_sb[g][:, i, :].rearrange("p (j d) -> p d j", j=PACK))
+            live["grouped_v", h] = grouped_v
+
+        def quantise_v_2(h):
+            cols = slice(h * D, (h + 1) * D)
             nc.vector.quantize_mx(
                 out=v_codes[:, cols].bitcast(FP8X4),
                 scales=v_scales[:, cols],
-                in_=grouped_v[:].rearrange("p g d j -> p (g d j)"),
+                in_=live["grouped_v", h][:].rearrange("p d j -> p (d j)"),
             )
 
         def transpose_q_k(h):
@@ -109,65 +109,85 @@ def tile_modelnew_t_kernel(tc, q, k, v, out):
                 nc.tensor.transpose(
                     qk_ps[:, S + j * P : S + (j + 1) * P], k_sb[g][:, i, j * D : (j + 1) * D], ident_bf[:]
                 )
-            qk_t = work.tile([P, 2 * S], BF16, tag="qk_t")
-            nc.scalar.copy(out=qk_t[:], in_=qk_ps[:])
-            transposed[h] = qk_t
+            live["qk_ps", h] = qk_ps
 
-        def scores_and_squares(h):
-            qk_t = transposed[h]
+        def copy_q_k(h):
+            qk_t = work.tile([P, 2 * S], BF16, tag="qk_t")
+            nc.scalar.copy(out=qk_t[:], in_=live["qk_ps", h][:])
+            live["qk_t", h] = qk_t
+
+        def scores(h):
+            qk_t = live["qk_t", h]
             k_t = qk_t[:, S : 2 * S].rearrange("d (j p) -> d j p", j=PACK)
-            s2 = squares[h % SLOTS][:].rearrange("m (c u x) -> m c u x", c=CHUNKS, u=2)
-            z = row_sums[h % SLOTS]
             diag_ps = psum.tile([P, S], F32, tag="diag_ps")
             past_a = psum.tile([P, S], F32, tag="past_a")
             past_b = psum.tile([P, 2 * P], F32, tag="past_b")
             past = {1: past_a[:, 0:P], 3: past_a[:, P : 4 * P], 2: past_b[:, 0 : 2 * P]}
+            for c in range(1, CHUNKS):
+                nc.tensor.matmul(
+                    out=past[c].rearrange("m (j w) -> m j w", j=PACK),
+                    lhsT=qk_t[:, c * P : (c + 1) * P],
+                    rhs=k_t[:, :, 0 : c * QUARTER],
+                    start=True,
+                    stop=True,
+                )
             for c in range(CHUNKS):
-                q_t = qk_t[:, c * P : (c + 1) * P]
                 nc.tensor.matmul(
                     out=diag_ps[:, c * P : (c + 1) * P].rearrange("m (j w) -> m j w", j=PACK),
-                    lhsT=q_t,
+                    lhsT=qk_t[:, c * P : (c + 1) * P],
                     rhs=k_t[:, :, c * QUARTER : (c + 1) * QUARTER],
                     start=True,
                     stop=True,
                 )
-                if c > 0:
-                    nc.tensor.matmul(
-                        out=past[c].rearrange("m (j w) -> m j w", j=PACK),
-                        lhsT=q_t,
-                        rhs=k_t[:, :, 0 : c * QUARTER],
-                        start=True,
-                        stop=True,
-                    )
+            live["diag_ps", h] = diag_ps
+            live["past", h] = past
+
+        def mask_diagonal(h):
             masked = work.tile([P, S], F32, tag="masked")
             nc.vector.tensor_tensor(
                 out=masked[:].rearrange("m (c x) -> m c x", c=CHUNKS),
-                in0=diag_ps[:].rearrange("m (c x) -> m c x", c=CHUNKS),
+                in0=live["diag_ps", h][:].rearrange("m (c x) -> m c x", c=CHUNKS),
                 in1=causal_jw[:].unsqueeze(1).to_broadcast([P, CHUNKS, P]),
                 op=ALU.mult,
             )
-            for c in range(CHUNKS):
-                seen = 2 * c * QUARTER
-                if c > 0:
-                    nc.scalar.activation(
-                        out=s2[:, c, :, 0:seen].rearrange("m u (w e) -> m u w e", e=2),
-                        in_=past[c].rearrange("m (u e w) -> m u w e", u=2, e=2),
-                        func=ACT.Square,
-                        scale=SCALE,
-                        accum_out=z[:, c : c + 1],
-                    )
-                nc.scalar.activation(
-                    out=s2[:, c, :, seen : seen + 2 * QUARTER].rearrange("m u (w e) -> m u w e", e=2),
-                    in_=masked[:, c * P : (c + 1) * P].rearrange("m (u e w) -> m u w e", u=2, e=2),
-                    func=ACT.Square,
-                    scale=SCALE,
-                    accum_out=z[:, CHUNKS + c : CHUNKS + c + 1],
-                )
+            live["masked", h] = masked
 
-        def transpose_and_quantise(h):
+        def square(h, c, scores_jw, first_column, z_column):
+            width = scores_jw.shape[1] // 2
+            s2 = squares[h % SLOTS][:].rearrange("m (c u x) -> m c u x", c=CHUNKS, u=2)
+            nc.scalar.activation(
+                out=s2[:, c, :, first_column : first_column + width].rearrange("m u (w e) -> m u w e", e=2),
+                in_=scores_jw.rearrange("m (u e w) -> m u w e", u=2, e=2),
+                func=ACT.Square,
+                scale=SCALE,
+                accum_out=row_sums[h % SLOTS][:, z_column : z_column + 1],
+            )
+
+        def square_past(h):
+            for c in range(1, CHUNKS):
+                square(h, c, live["past", h][c], 0, c)
+
+        def square_diagonal(h):
+            for c in range(CHUNKS):
+                square(h, c, live["masked", h][:, c * P : (c + 1) * P], 2 * c * QUARTER, CHUNKS + c)
+
+        def invert_row_sums(h):
+            z = row_sums[h % SLOTS]
+            denom = work.tile([P, CHUNKS], F32, tag="denom")
+            nc.vector.scalar_tensor_tensor(
+                out=denom[:],
+                in0=z[:, 0:CHUNKS],
+                scalar=EPS,
+                in1=z[:, CHUNKS : 2 * CHUNKS],
+                op0=ALU.add,
+                op1=ALU.add,
+            )
+            inverse = work.tile([P, CHUNKS], F32, tag="inverse", bufs=4)
+            nc.vector.reciprocal(out=inverse[:], in_=denom[:])
+            live["inverse", h] = inverse
+
+        def transpose_squares(h):
             words = squares[h % SLOTS][:].bitcast(F32)
-            grouped = work.tile([P, CHUNKS * P * PACK], BF16, align_bytes=64, tag="grouped")
-            grouped_words = grouped[:].bitcast(F32)
             for half in range(2):
                 s2t_ps = psum.tile([P, S], F32, tag="s2t_ps", bufs=3)
                 for n in range(4):
@@ -175,18 +195,27 @@ def tile_modelnew_t_kernel(tc, q, k, v, out):
                     nc.tensor.transpose(
                         s2t_ps[:, n * P : (n + 1) * P], words[:, plane * P : (plane + 1) * P], ident_f32[:]
                     )
-                nc.vector.tensor_copy(
-                    out=grouped_words[:, half * S : (half + 1) * S].rearrange("p (c m u) -> p c m u", c=2, u=2),
-                    in_=s2t_ps[:].rearrange("p (c u m) -> p c m u", c=2, u=2),
-                )
+                live["s2t_ps", h, half] = s2t_ps
+
+        def copy_squares(h, half, copy):
+            if half == 0:
+                grouped = work.tile([P, CHUNKS * P * PACK], BF16, align_bytes=64, tag="grouped")
+                live["grouped", h] = grouped
+            copy(
+                out=live["grouped", h][:]
+                .bitcast(F32)[:, half * S : (half + 1) * S]
+                .rearrange("p (c m u) -> p c m u", c=2, u=2),
+                in_=live["s2t_ps", h, half][:].rearrange("p (c u m) -> p c m u", c=2, u=2),
+            )
+
+        def quantise_squares(h):
             codes = work.tile([P, S], U32, align_bytes=64, tag="codes")
             scales = work.tile([P, S], U8, align_bytes=64, tag="scales")
-            nc.vector.quantize_mx(out=codes[:].bitcast(FP8X4), scales=scales[:], in_=grouped[:])
-            quantised[h] = (codes, scales)
+            nc.vector.quantize_mx(out=codes[:].bitcast(FP8X4), scales=scales[:], in_=live["grouped", h][:])
+            live["codes", h] = (codes, scales)
 
         def weighted_values(h):
-            codes, scales = quantised[h]
-            z = row_sums[h % SLOTS]
+            codes, scales = live["codes", h]
             o_ps = psum.tile([P, S], F32, tag="o_ps")
             v_cols = slice(h * D, (h + 1) * D)
             for c in range(CHUNKS):
@@ -200,35 +229,37 @@ def tile_modelnew_t_kernel(tc, q, k, v, out):
                     start=True,
                     stop=True,
                 )
-            denom = work.tile([P, CHUNKS], F32, tag="denom")
-            nc.vector.scalar_tensor_tensor(
-                out=denom[:],
-                in0=z[:, 0:CHUNKS],
-                scalar=EPS,
-                in1=z[:, CHUNKS : 2 * CHUNKS],
-                op0=ALU.add,
-                op1=ALU.add,
-            )
-            inverse = work.tile([P, CHUNKS], F32, tag="inverse")
-            nc.vector.reciprocal(out=inverse[:], in_=denom[:])
-            o_sb = work.tile([P, CHUNKS, D], F32, tag="o_sb", bufs=4)
-            for c in range(CHUNKS):
-                nc.scalar.activation(
-                    out=o_sb[:, c, :],
-                    in_=o_ps[:, c * P : (c + 1) * P],
-                    func=ACT.Copy,
-                    scale=inverse[:, c : c + 1],
-                )
-            nc.sync.dma_start(out=out_rows[:, h, :, :], in_=o_sb[:])
+            live["o_ps", h] = o_ps
 
-        for step in range(HEADS + 3):
-            if step < HEADS:
-                if step % GROUP == 0:
-                    quantise_v(step // GROUP)
-                transpose_q_k(step)
-            if 0 <= step - 1 < HEADS:
-                scores_and_squares(step - 1)
-            if 0 <= step - 2 < HEADS:
-                transpose_and_quantise(step - 2)
-            if 0 <= step - 3 < HEADS:
-                weighted_values(step - 3)
+        def divide_and_store(h):
+            o_sb = work.tile([P, CHUNKS, D], F32, tag="o_sb", bufs=4)
+            nc.vector.tensor_tensor(
+                out=o_sb[:],
+                in0=live["o_ps", h][:].rearrange("m (c d) -> m c d", c=CHUNKS),
+                in1=live["inverse", h][:].unsqueeze(2).to_broadcast([P, CHUNKS, D]),
+                op=ALU.mult,
+            )
+            nc.gpsimd.dma_start(out=out_rows[:, h, :, :], in_=o_sb[:])
+
+        def when(h, stage, *more):
+            if 0 <= h < HEADS:
+                stage(h, *more)
+
+        with tc.manual_schedule():
+            transpose_q_k(0)
+            for r in range(HEADS + 4):
+                when(r - 1, mask_diagonal)
+                when(r - 1, square_past)
+                when(r, copy_q_k)
+                when(r - 4, divide_and_store)
+                when(r, quantise_v)
+                when(r - 3, quantise_squares)
+                when(r - 1, square_diagonal)
+                when(r - 2, invert_row_sums)
+                when(r, quantise_v_2)
+                when(r - 2, copy_squares, 0, nc.vector.tensor_copy)
+                when(r - 2, copy_squares, 1, nc.scalar.copy)
+                when(r, scores)
+                when(r - 3, weighted_values)
+                when(r + 1, transpose_q_k)
+                when(r - 1, transpose_squares)

@@ -17,8 +17,8 @@ P = 128
 CHUNKS = S // P
 PACK = 4
 QUARTER = P // PACK
-GROUP = 2
-SLOTS = 3
+GROUP = 4
+SLOTS = 4
 EPS = 1e-6
 SCALE = D ** -0.5
 
@@ -60,6 +60,9 @@ def tile_modelnew_t_kernel(tc, q, k, v, out):
             in_=causal[:].rearrange("m (w j) -> m j w", j=PACK),
         )
 
+        minus_one = const.tile([P, CHUNKS], F32)
+        nc.gpsimd.memset(minus_one[:], -1.0)
+
         q_sb, k_sb, v_sb = [], [], []
         for g in range(HEADS // GROUP):
             heads = slice(g * GROUP, (g + 1) * GROUP)
@@ -84,20 +87,20 @@ def tile_modelnew_t_kernel(tc, q, k, v, out):
             squares.append(s2)
             row_sums.append(z)
 
-        live = {}
+        transposed = {}
+        quantised = {}
 
-        def quantise_v(h):
-            g, i = divmod(h, GROUP)
-            grouped_v = work.tile([P, D, PACK], BF16, align_bytes=64, tag="grouped_v")
-            nc.vector.tensor_copy(out=grouped_v[:], in_=v_sb[g][:, i, :].rearrange("p (j d) -> p d j", j=PACK))
-            live["grouped_v", h] = grouped_v
-
-        def quantise_v_2(h):
-            cols = slice(h * D, (h + 1) * D)
+        def quantise_v(g):
+            grouped_v = work.tile([P, GROUP, D, PACK], BF16, align_bytes=64, tag="grouped_v", bufs=2)
+            nc.vector.tensor_copy(
+                out=grouped_v[:],
+                in_=v_sb[g][:].rearrange("p g (j d) -> p g d j", j=PACK),
+            )
+            cols = slice(g * GROUP * D, (g + 1) * GROUP * D)
             nc.vector.quantize_mx(
                 out=v_codes[:, cols].bitcast(FP8X4),
                 scales=v_scales[:, cols],
-                in_=live["grouped_v", h][:].rearrange("p d j -> p (d j)"),
+                in_=grouped_v[:].rearrange("p g d j -> p (g d j)"),
             )
 
         def transpose_q_k(h):
@@ -109,85 +112,65 @@ def tile_modelnew_t_kernel(tc, q, k, v, out):
                 nc.tensor.transpose(
                     qk_ps[:, S + j * P : S + (j + 1) * P], k_sb[g][:, i, j * D : (j + 1) * D], ident_bf[:]
                 )
-            live["qk_ps", h] = qk_ps
-
-        def copy_q_k(h):
             qk_t = work.tile([P, 2 * S], BF16, tag="qk_t")
-            nc.scalar.copy(out=qk_t[:], in_=live["qk_ps", h][:])
-            live["qk_t", h] = qk_t
+            nc.scalar.copy(out=qk_t[:], in_=qk_ps[:])
+            transposed[h] = qk_t
 
-        def scores(h):
-            qk_t = live["qk_t", h]
+        def scores_and_squares(h):
+            qk_t = transposed[h]
             k_t = qk_t[:, S : 2 * S].rearrange("d (j p) -> d j p", j=PACK)
+            s2 = squares[h % SLOTS][:].rearrange("m (c u x) -> m c u x", c=CHUNKS, u=2)
+            z = row_sums[h % SLOTS]
             diag_ps = psum.tile([P, S], F32, tag="diag_ps")
             past_a = psum.tile([P, S], F32, tag="past_a")
             past_b = psum.tile([P, 2 * P], F32, tag="past_b")
             past = {1: past_a[:, 0:P], 3: past_a[:, P : 4 * P], 2: past_b[:, 0 : 2 * P]}
-            for c in range(1, CHUNKS):
-                nc.tensor.matmul(
-                    out=past[c].rearrange("m (j w) -> m j w", j=PACK),
-                    lhsT=qk_t[:, c * P : (c + 1) * P],
-                    rhs=k_t[:, :, 0 : c * QUARTER],
-                    start=True,
-                    stop=True,
-                )
             for c in range(CHUNKS):
+                q_t = qk_t[:, c * P : (c + 1) * P]
                 nc.tensor.matmul(
                     out=diag_ps[:, c * P : (c + 1) * P].rearrange("m (j w) -> m j w", j=PACK),
-                    lhsT=qk_t[:, c * P : (c + 1) * P],
+                    lhsT=q_t,
                     rhs=k_t[:, :, c * QUARTER : (c + 1) * QUARTER],
                     start=True,
                     stop=True,
                 )
-            live["diag_ps", h] = diag_ps
-            live["past", h] = past
-
-        def mask_diagonal(h):
+                if c > 0:
+                    nc.tensor.matmul(
+                        out=past[c].rearrange("m (j w) -> m j w", j=PACK),
+                        lhsT=q_t,
+                        rhs=k_t[:, :, 0 : c * QUARTER],
+                        start=True,
+                        stop=True,
+                    )
             masked = work.tile([P, S], F32, tag="masked")
             nc.vector.tensor_tensor(
                 out=masked[:].rearrange("m (c x) -> m c x", c=CHUNKS),
-                in0=live["diag_ps", h][:].rearrange("m (c x) -> m c x", c=CHUNKS),
+                in0=diag_ps[:].rearrange("m (c x) -> m c x", c=CHUNKS),
                 in1=causal_jw[:].unsqueeze(1).to_broadcast([P, CHUNKS, P]),
                 op=ALU.mult,
             )
-            live["masked", h] = masked
-
-        def square(h, c, scores_jw, first_column, z_column):
-            width = scores_jw.shape[1] // 2
-            s2 = squares[h % SLOTS][:].rearrange("m (c u x) -> m c u x", c=CHUNKS, u=2)
-            nc.scalar.activation(
-                out=s2[:, c, :, first_column : first_column + width].rearrange("m u (w e) -> m u w e", e=2),
-                in_=scores_jw.rearrange("m (u e w) -> m u w e", u=2, e=2),
-                func=ACT.Square,
-                scale=SCALE,
-                accum_out=row_sums[h % SLOTS][:, z_column : z_column + 1],
-            )
-
-        def square_past(h):
-            for c in range(1, CHUNKS):
-                square(h, c, live["past", h][c], 0, c)
-
-        def square_diagonal(h):
             for c in range(CHUNKS):
-                square(h, c, live["masked", h][:, c * P : (c + 1) * P], 2 * c * QUARTER, CHUNKS + c)
+                seen = 2 * c * QUARTER
+                if c > 0:
+                    nc.scalar.activation(
+                        out=s2[:, c, :, 0:seen].rearrange("m u (w e) -> m u w e", e=2),
+                        in_=past[c].rearrange("m (u e w) -> m u w e", u=2, e=2),
+                        func=ACT.Square,
+                        scale=SCALE,
+                        accum_out=z[:, c : c + 1],
+                    )
+                nc.scalar.activation(
+                    out=s2[:, c, :, seen : seen + 2 * QUARTER].rearrange("m u (w e) -> m u w e", e=2),
+                    in_=masked[:, c * P : (c + 1) * P].rearrange("m (u e w) -> m u w e", u=2, e=2),
+                    func=ACT.Square,
+                    scale=SCALE,
+                    accum_out=z[:, CHUNKS + c : CHUNKS + c + 1],
+                )
 
-        def invert_row_sums(h):
-            z = row_sums[h % SLOTS]
-            denom = work.tile([P, CHUNKS], F32, tag="denom")
-            nc.vector.scalar_tensor_tensor(
-                out=denom[:],
-                in0=z[:, 0:CHUNKS],
-                scalar=EPS,
-                in1=z[:, CHUNKS : 2 * CHUNKS],
-                op0=ALU.add,
-                op1=ALU.add,
-            )
-            inverse = work.tile([P, CHUNKS], F32, tag="inverse", bufs=4)
-            nc.vector.reciprocal(out=inverse[:], in_=denom[:])
-            live["inverse", h] = inverse
-
-        def transpose_squares(h):
+        def transpose_and_quantise(h):
             words = squares[h % SLOTS][:].bitcast(F32)
+            grouped = work.tile([P, CHUNKS * P * PACK], BF16, align_bytes=64, tag="grouped")
+            grouped_words = grouped[:].bitcast(F32)
             for half in range(2):
                 s2t_ps = psum.tile([P, S], F32, tag="s2t_ps", bufs=3)
                 for n in range(4):
@@ -195,27 +178,19 @@ def tile_modelnew_t_kernel(tc, q, k, v, out):
                     nc.tensor.transpose(
                         s2t_ps[:, n * P : (n + 1) * P], words[:, plane * P : (plane + 1) * P], ident_f32[:]
                     )
-                live["s2t_ps", h, half] = s2t_ps
-
-        def copy_squares(h, half, copy):
-            if half == 0:
-                grouped = work.tile([P, CHUNKS * P * PACK], BF16, align_bytes=64, tag="grouped")
-                live["grouped", h] = grouped
-            copy(
-                out=live["grouped", h][:]
-                .bitcast(F32)[:, half * S : (half + 1) * S]
-                .rearrange("p (c m u) -> p c m u", c=2, u=2),
-                in_=live["s2t_ps", h, half][:].rearrange("p (c u m) -> p c m u", c=2, u=2),
-            )
-
-        def quantise_squares(h):
+                copy = nc.scalar.copy if (half == 1 and h % 2 == 1) else nc.vector.tensor_copy
+                copy(
+                    out=grouped_words[:, half * S : (half + 1) * S].rearrange("p (c m u) -> p c m u", c=2, u=2),
+                    in_=s2t_ps[:].rearrange("p (c u m) -> p c m u", c=2, u=2),
+                )
             codes = work.tile([P, S], U32, align_bytes=64, tag="codes")
             scales = work.tile([P, S], U8, align_bytes=64, tag="scales")
-            nc.vector.quantize_mx(out=codes[:].bitcast(FP8X4), scales=scales[:], in_=live["grouped", h][:])
-            live["codes", h] = (codes, scales)
+            nc.vector.quantize_mx(out=codes[:].bitcast(FP8X4), scales=scales[:], in_=grouped[:])
+            quantised[h] = (codes, scales)
 
         def weighted_values(h):
-            codes, scales = live["codes", h]
+            codes, scales = quantised[h]
+            z = row_sums[h % SLOTS]
             o_ps = psum.tile([P, S], F32, tag="o_ps")
             v_cols = slice(h * D, (h + 1) * D)
             for c in range(CHUNKS):
@@ -229,37 +204,29 @@ def tile_modelnew_t_kernel(tc, q, k, v, out):
                     start=True,
                     stop=True,
                 )
-            live["o_ps", h] = o_ps
-
-        def divide_and_store(h):
+            denom = work.tile([P, CHUNKS], F32, tag="denom")
+            nc.gpsimd.tensor_tensor(out=denom[:], in0=z[:, 0:CHUNKS], in1=z[:, CHUNKS : 2 * CHUNKS], op=ALU.add)
+            inverse = work.tile([P, CHUNKS], F32, tag="inverse")
+            nc.gpsimd.tensor_scalar(out=denom[:], in0=denom[:], scalar1=EPS, scalar2=0.0, op0=ALU.add, op1=ALU.add)
+            nc.gpsimd.tensor_tensor(out=inverse[:], in0=denom[:], in1=minus_one[:], op=ALU.pow)
             o_sb = work.tile([P, CHUNKS, D], F32, tag="o_sb", bufs=4)
-            nc.vector.tensor_tensor(
-                out=o_sb[:],
-                in0=live["o_ps", h][:].rearrange("m (c d) -> m c d", c=CHUNKS),
-                in1=live["inverse", h][:].unsqueeze(2).to_broadcast([P, CHUNKS, D]),
-                op=ALU.mult,
-            )
-            nc.gpsimd.dma_start(out=out_rows[:, h, :, :], in_=o_sb[:])
+            for c in range(CHUNKS):
+                nc.scalar.activation(
+                    out=o_sb[:, c, :],
+                    in_=o_ps[:, c * P : (c + 1) * P],
+                    func=ACT.Copy,
+                    scale=inverse[:, c : c + 1],
+                )
+            nc.sync.dma_start(out=out_rows[:, h, :, :], in_=o_sb[:])
 
-        def when(h, stage, *more):
-            if 0 <= h < HEADS:
-                stage(h, *more)
-
-        with tc.manual_schedule():
-            transpose_q_k(0)
-            for r in range(HEADS + 4):
-                when(r - 1, mask_diagonal)
-                when(r - 1, square_past)
-                when(r, copy_q_k)
-                when(r - 4, divide_and_store)
-                when(r, quantise_v)
-                when(r - 3, quantise_squares)
-                when(r - 1, square_diagonal)
-                when(r - 2, invert_row_sums)
-                when(r, quantise_v_2)
-                when(r - 2, copy_squares, 0, nc.vector.tensor_copy)
-                when(r - 2, copy_squares, 1, nc.scalar.copy)
-                when(r, scores)
-                when(r - 3, weighted_values)
-                when(r + 1, transpose_q_k)
-                when(r - 1, transpose_squares)
+        for step in range(HEADS + 3):
+            if step < HEADS:
+                if step % GROUP == 0:
+                    quantise_v(step // GROUP)
+                transpose_q_k(step)
+            if 0 <= step - 1 < HEADS:
+                scores_and_squares(step - 1)
+            if 0 <= step - 2 < HEADS:
+                transpose_and_quantise(step - 2)
+            if 0 <= step - 3 < HEADS:
+                weighted_values(step - 3)

@@ -60,28 +60,31 @@ def tile_modelnew_t_kernel(tc, q, k, v, out):
             in_=causal[:].rearrange("m (w j) -> m j w", j=PACK),
         )
 
-        minus_one = const.tile([P, CHUNKS], F32)
-        nc.gpsimd.memset(minus_one[:], -1.0)
-
-        q_sb, k_sb, v_sb = [], [], []
-        for g in range(HEADS // GROUP):
-            heads = slice(g * GROUP, (g + 1) * GROUP)
-            q_g = loads.tile([P, GROUP * CHUNKS, D], BF16, name="q_g%d" % g)
-            nc.sync.dma_start(out=q_g[:], in_=q_rows[:, g * GROUP * CHUNKS : (g + 1) * GROUP * CHUNKS, :])
-            k_g = loads.tile([P, GROUP, PACK * D], BF16, name="k_g%d" % g)
-            nc.sync.dma_start(out=k_g[:], in_=k_rows[:, heads, :])
-            v_g = loads.tile([P, GROUP, PACK * D], BF16, name="v_g%d" % g)
-            nc.sync.dma_start(out=v_g[:], in_=v_rows[:, heads, :])
-            q_sb.append(q_g)
-            k_sb.append(k_g)
-            v_sb.append(v_g)
+        groups = []
+        loaded = 0
+        while loaded < HEADS:
+            groups.append((loaded, min(GROUP, max(1, loaded))))
+            loaded += groups[-1][1]
+        q_sb, k_sb = {}, {}
+        v_group = {}
+        for first, n in groups:
+            q_g = loads.tile([P, n * CHUNKS, D], BF16, name="q_g%d" % first)
+            nc.sync.dma_start(out=q_g[:], in_=q_rows[:, first * CHUNKS : (first + n) * CHUNKS, :])
+            k_g = loads.tile([P, n, PACK * D], BF16, name="k_g%d" % first)
+            nc.sync.dma_start(out=k_g[:], in_=k_rows[:, first : first + n, :])
+            v_g = loads.tile([P, n, PACK * D], BF16, name="v_g%d" % first)
+            nc.sync.dma_start(out=v_g[:], in_=v_rows[:, first : first + n, :])
+            v_group[first] = (v_g, n)
+            for i in range(n):
+                q_sb[first + i] = q_g[:, i * CHUNKS : (i + 1) * CHUNKS, :]
+                k_sb[first + i] = k_g[:, i, :]
 
         v_codes = keep.tile([P, HEADS * D], U32, align_bytes=64)
         v_scales = keep.tile([P, HEADS * D], U8, align_bytes=64)
         squares, row_sums = [], []
         for slot in range(SLOTS):
             s2 = keep.tile([P, CHUNKS * S], BF16, name="s2_%d" % slot)
-            nc.vector.memset(s2[:], 0.0)
+            nc.gpsimd.memset(s2[:].bitcast(F32), 0.0)
             z = keep.tile([P, 2 * CHUNKS], F32, name="z_%d" % slot)
             nc.vector.memset(z[:], 0.0)
             squares.append(s2)
@@ -90,13 +93,11 @@ def tile_modelnew_t_kernel(tc, q, k, v, out):
         transposed = {}
         quantised = {}
 
-        def quantise_v(g):
-            grouped_v = work.tile([P, GROUP, D, PACK], BF16, align_bytes=64, tag="grouped_v", bufs=2)
-            nc.vector.tensor_copy(
-                out=grouped_v[:],
-                in_=v_sb[g][:].rearrange("p g (j d) -> p g d j", j=PACK),
-            )
-            cols = slice(g * GROUP * D, (g + 1) * GROUP * D)
+        def quantise_v(first):
+            v_g, n = v_group[first]
+            grouped_v = work.tile([P, n, D, PACK], BF16, align_bytes=64, tag="grouped_v", bufs=2)
+            nc.vector.tensor_copy(out=grouped_v[:], in_=v_g[:].rearrange("p g (j d) -> p g d j", j=PACK))
+            cols = slice(first * D, (first + n) * D)
             nc.vector.quantize_mx(
                 out=v_codes[:, cols].bitcast(FP8X4),
                 scales=v_scales[:, cols],
@@ -104,16 +105,15 @@ def tile_modelnew_t_kernel(tc, q, k, v, out):
             )
 
         def transpose_q_k(h):
-            g, i = divmod(h, GROUP)
             qk_ps = psum.tile([P, 2 * S], BF16, tag="qk_ps")
             for c in range(CHUNKS):
-                nc.tensor.transpose(qk_ps[:, c * P : (c + 1) * P], q_sb[g][:, i * CHUNKS + c, :], ident_bf[:])
+                nc.tensor.transpose(qk_ps[:, c * P : (c + 1) * P], q_sb[h][:, c, :], ident_bf[:])
             for j in range(PACK):
                 nc.tensor.transpose(
-                    qk_ps[:, S + j * P : S + (j + 1) * P], k_sb[g][:, i, j * D : (j + 1) * D], ident_bf[:]
+                    qk_ps[:, S + j * P : S + (j + 1) * P], k_sb[h][:, j * D : (j + 1) * D], ident_bf[:]
                 )
             qk_t = work.tile([P, 2 * S], BF16, tag="qk_t")
-            nc.scalar.copy(out=qk_t[:], in_=qk_ps[:])
+            nc.vector.tensor_copy(out=qk_t[:], in_=qk_ps[:])
             transposed[h] = qk_t
 
         def scores_and_squares(h):
@@ -178,7 +178,7 @@ def tile_modelnew_t_kernel(tc, q, k, v, out):
                     nc.tensor.transpose(
                         s2t_ps[:, n * P : (n + 1) * P], words[:, plane * P : (plane + 1) * P], ident_f32[:]
                     )
-                copy = nc.scalar.copy if (half == 1 and h % 2 == 1) else nc.vector.tensor_copy
+                copy = nc.vector.tensor_copy if half == 0 else nc.scalar.copy
                 copy(
                     out=grouped_words[:, half * S : (half + 1) * S].rearrange("p (c m u) -> p c m u", c=2, u=2),
                     in_=s2t_ps[:].rearrange("p (c u m) -> p c m u", c=2, u=2),
@@ -205,11 +205,17 @@ def tile_modelnew_t_kernel(tc, q, k, v, out):
                     stop=True,
                 )
             denom = work.tile([P, CHUNKS], F32, tag="denom")
-            nc.gpsimd.tensor_tensor(out=denom[:], in0=z[:, 0:CHUNKS], in1=z[:, CHUNKS : 2 * CHUNKS], op=ALU.add)
+            nc.vector.scalar_tensor_tensor(
+                out=denom[:],
+                in0=z[:, 0:CHUNKS],
+                scalar=EPS,
+                in1=z[:, CHUNKS : 2 * CHUNKS],
+                op0=ALU.add,
+                op1=ALU.add,
+            )
             inverse = work.tile([P, CHUNKS], F32, tag="inverse")
-            nc.gpsimd.tensor_scalar(out=denom[:], in0=denom[:], scalar1=EPS, scalar2=0.0, op0=ALU.add, op1=ALU.add)
-            nc.gpsimd.tensor_tensor(out=inverse[:], in0=denom[:], in1=minus_one[:], op=ALU.pow)
-            o_sb = work.tile([P, CHUNKS, D], F32, tag="o_sb", bufs=4)
+            nc.vector.reciprocal(out=inverse[:], in_=denom[:])
+            o_sb = work.tile([P, CHUNKS, D], F32, tag="o_sb", bufs=8)
             for c in range(CHUNKS):
                 nc.scalar.activation(
                     out=o_sb[:, c, :],
@@ -221,11 +227,11 @@ def tile_modelnew_t_kernel(tc, q, k, v, out):
 
         for step in range(HEADS + 3):
             if step < HEADS:
-                if step % GROUP == 0:
-                    quantise_v(step // GROUP)
                 transpose_q_k(step)
             if 0 <= step - 1 < HEADS:
                 scores_and_squares(step - 1)
+                if step - 1 in v_group:
+                    quantise_v(step - 1)
             if 0 <= step - 2 < HEADS:
                 transpose_and_quantise(step - 2)
             if 0 <= step - 3 < HEADS:

@@ -14,23 +14,59 @@ ALU = mybir.AluOpType
 B, H, S, D = 4, 8, 512, 128
 HEADS = B * H
 P = 128
-CHUNKS = S // P
+CHUNKS = 4
 PACK = 4
 QUARTER = P // PACK
+TILES = 5
+LAST = CHUNKS - 1
 GROUP = 4
-SLOTS = 4
+PAIR_SLOTS = 4
+V_SLOTS = 8
 EPS = 1e-6
 SCALE = D ** -0.5
 
 FLOPS = 2 * (2 * HEADS * S * S * D)
 
 
+def diag_rows(h, c):
+    if h % 2 == 0:
+        return c * QUARTER, (c + 1) * QUARTER
+    return (LAST - c) * QUARTER, (CHUNKS - c) * QUARTER
+
+
+def past_rows(h, c):
+    if h % 2 == 0:
+        return 0, c * QUARTER
+    return (CHUNKS - c) * QUARTER, P
+
+
+def seen_rows(h, c):
+    if h % 2 == 0:
+        return 0, (c + 1) * QUARTER
+    return (LAST - c) * QUARTER, P
+
+
+def tile_of(h, c):
+    if c == LAST:
+        return h % 2
+    return 2 + (c if h % 2 == 0 else LAST - 1 - c)
+
+
 def tile_modelnew_t_kernel(tc, q, k, v, out):
     nc = tc.nc
     q_rows = q.rearrange("b h (c m) d -> m (b h c) d", m=P)
-    k_rows = k.rearrange("b h (p j) d -> p (b h) (j d)", j=PACK)
-    v_rows = v.rearrange("b h (p j) d -> p (b h) (j d)", j=PACK)
     out_rows = out.rearrange("b h (c m) d -> m (b h) c d", m=P)
+
+    def by_partition(x):
+        return x.rearrange("b h (p j) d -> p (b h) (j d)", j=PACK)
+
+    def by_group(x):
+        return [
+            x[:, :, g * P : (g + 1) * P, :].rearrange("b h (r j) d -> r (b h) (j d)", j=PACK) for g in range(CHUNKS)
+        ]
+
+    k_rows, v_rows = by_partition(k), by_partition(v)
+    k_groups, v_groups = by_group(k), by_group(v)
 
     with ExitStack() as ctx:
         const = ctx.enter_context(tc.tile_pool(name="const", bufs=1))
@@ -60,20 +96,26 @@ def tile_modelnew_t_kernel(tc, q, k, v, out):
             in_=causal[:].rearrange("m (w j) -> m j w", j=PACK),
         )
 
-        groups = []
+        def load_keys(dst, rows, groups, first, n):
+            nc.sync.dma_start(out=dst[:, 0:n:2, :], in_=rows[:, first : first + n : 2, :])
+            for g in range(CHUNKS):
+                lo, hi = diag_rows(1, g)
+                nc.sync.dma_start(out=dst[lo:hi, 1:n:2, :], in_=groups[g][:, first + 1 : first + n : 2, :])
+
+        groups_of_heads = []
         loaded = 0
         while loaded < HEADS:
-            groups.append((loaded, min(GROUP, max(1, loaded))))
-            loaded += groups[-1][1]
+            groups_of_heads.append((loaded, min(GROUP, max(2, loaded))))
+            loaded += groups_of_heads[-1][1]
         q_sb, k_sb = {}, {}
         v_group = {}
-        for first, n in groups:
+        for first, n in groups_of_heads:
             q_g = loads.tile([P, n * CHUNKS, D], BF16, name="q_g%d" % first)
             nc.sync.dma_start(out=q_g[:], in_=q_rows[:, first * CHUNKS : (first + n) * CHUNKS, :])
             k_g = loads.tile([P, n, PACK * D], BF16, name="k_g%d" % first)
-            nc.sync.dma_start(out=k_g[:], in_=k_rows[:, first : first + n, :])
+            load_keys(k_g, k_rows, k_groups, first, n)
             v_g = loads.tile([P, n, PACK * D], BF16, name="v_g%d" % first)
-            nc.sync.dma_start(out=v_g[:], in_=v_rows[:, first : first + n, :])
+            load_keys(v_g, v_rows, v_groups, first, n)
             v_group[first] = (v_g, n)
             for i in range(n):
                 q_sb[first + i] = q_g[:, i * CHUNKS : (i + 1) * CHUNKS, :]
@@ -81,16 +123,16 @@ def tile_modelnew_t_kernel(tc, q, k, v, out):
 
         v_codes = keep.tile([P, HEADS * D], U32, align_bytes=64)
         v_scales = keep.tile([P, HEADS * D], U8, align_bytes=64)
-        squares, row_sums = [], []
-        for slot in range(SLOTS):
-            s2 = keep.tile([P, CHUNKS * S], BF16, name="s2_%d" % slot)
-            nc.gpsimd.memset(s2[:].bitcast(F32), 0.0)
-            z = keep.tile([P, 2 * CHUNKS], F32, name="z_%d" % slot)
+        masked_v = keep.tile([P, V_SLOTS * LAST * D], U32, align_bytes=64)
+        nc.gpsimd.memset(masked_v[:].bitcast(F32), 0.0)
+        row_sums = []
+        for slot in range(PAIR_SLOTS):
+            z = keep.tile([P, 2 * 2 * CHUNKS], F32, name="z_%d" % slot)
             nc.vector.memset(z[:], 0.0)
-            squares.append(s2)
             row_sums.append(z)
 
         transposed = {}
+        squares = {}
         quantised = {}
 
         def quantise_v(first):
@@ -103,6 +145,18 @@ def tile_modelnew_t_kernel(tc, q, k, v, out):
                 scales=v_scales[:, cols],
                 in_=grouped_v[:].rearrange("p g d j -> p (g d j)"),
             )
+            by_head = v_codes[:].rearrange("p (h d) -> p h d", d=D)
+            by_slot = masked_v[:].rearrange("p (s c d) -> p s c d", c=LAST, d=D)
+            slot = first % V_SLOTS
+            for c in range(LAST):
+                for parity in range(2):
+                    lo, hi = seen_rows(parity, c)
+                    pieces = [(lo, hi)] if lo != QUARTER else [(lo, 2 * QUARTER), (2 * QUARTER, hi)]
+                    for a, b in pieces:
+                        nc.gpsimd.tensor_copy(
+                            out=by_slot[a:b, slot + parity : slot + n : 2, c, :],
+                            in_=by_head[a:b, first + parity : first + n : 2, :],
+                        )
 
         def transpose_q_k(h):
             qk_ps = psum.tile([P, 2 * S], BF16, tag="qk_ps")
@@ -119,29 +173,36 @@ def tile_modelnew_t_kernel(tc, q, k, v, out):
         def scores_and_squares(h):
             qk_t = transposed[h]
             k_t = qk_t[:, S : 2 * S].rearrange("d (j p) -> d j p", j=PACK)
-            s2 = squares[h % SLOTS][:].rearrange("m (c u x) -> m c u x", c=CHUNKS, u=2)
-            z = row_sums[h % SLOTS]
+            if h % 2 == 0:
+                s2_new = work.tile([P, TILES * 2 * 2 * P], BF16, tag="s2")
+                squares[h // 2] = s2_new
+            s2 = squares[h // 2][:].rearrange("m (t u x) -> m t u x", t=TILES, u=2)
+            z = row_sums[(h // 2) % PAIR_SLOTS]
+            z0 = (h % 2) * 2 * CHUNKS
             diag_ps = psum.tile([P, S], F32, tag="diag_ps")
             past_a = psum.tile([P, S], F32, tag="past_a")
             past_b = psum.tile([P, 2 * P], F32, tag="past_b")
             past = {1: past_a[:, 0:P], 3: past_a[:, P : 4 * P], 2: past_b[:, 0 : 2 * P]}
             for c in range(CHUNKS):
                 q_t = qk_t[:, c * P : (c + 1) * P]
+                lo, hi = diag_rows(h, c)
                 nc.tensor.matmul(
                     out=diag_ps[:, c * P : (c + 1) * P].rearrange("m (j w) -> m j w", j=PACK),
                     lhsT=q_t,
-                    rhs=k_t[:, :, c * QUARTER : (c + 1) * QUARTER],
+                    rhs=k_t[:, :, lo:hi],
                     start=True,
                     stop=True,
                 )
-                if c > 0:
-                    nc.tensor.matmul(
-                        out=past[c].rearrange("m (j w) -> m j w", j=PACK),
-                        lhsT=q_t,
-                        rhs=k_t[:, :, 0 : c * QUARTER],
-                        start=True,
-                        stop=True,
-                    )
+            for c in (1, 3, 2):
+                q_t = qk_t[:, c * P : (c + 1) * P]
+                lo, hi = past_rows(h, c)
+                nc.tensor.matmul(
+                    out=past[c].rearrange("m (j w) -> m j w", j=PACK),
+                    lhsT=q_t,
+                    rhs=k_t[:, :, lo:hi],
+                    start=True,
+                    stop=True,
+                )
             masked = work.tile([P, S], F32, tag="masked")
             nc.vector.tensor_tensor(
                 out=masked[:].rearrange("m (c x) -> m c x", c=CHUNKS),
@@ -149,81 +210,96 @@ def tile_modelnew_t_kernel(tc, q, k, v, out):
                 in1=causal_jw[:].unsqueeze(1).to_broadcast([P, CHUNKS, P]),
                 op=ALU.mult,
             )
-            for c in range(CHUNKS):
-                seen = 2 * c * QUARTER
-                if c > 0:
-                    nc.scalar.activation(
-                        out=s2[:, c, :, 0:seen].rearrange("m u (w e) -> m u w e", e=2),
-                        in_=past[c].rearrange("m (u e w) -> m u w e", u=2, e=2),
-                        func=ACT.Square,
-                        scale=SCALE,
-                        accum_out=z[:, c : c + 1],
-                    )
+            for c in (1, 3, 2):
+                lo, hi = past_rows(h, c)
                 nc.scalar.activation(
-                    out=s2[:, c, :, seen : seen + 2 * QUARTER].rearrange("m u (w e) -> m u w e", e=2),
+                    out=s2[:, tile_of(h, c), :, 2 * lo : 2 * hi].rearrange("m u (w e) -> m u w e", e=2),
+                    in_=past[c].rearrange("m (u e w) -> m u w e", u=2, e=2),
+                    func=ACT.Square,
+                    scale=SCALE,
+                    accum_out=z[:, z0 + c : z0 + c + 1],
+                )
+            for c in range(CHUNKS):
+                lo, hi = diag_rows(h, c)
+                nc.scalar.activation(
+                    out=s2[:, tile_of(h, c), :, 2 * lo : 2 * hi].rearrange("m u (w e) -> m u w e", e=2),
                     in_=masked[:, c * P : (c + 1) * P].rearrange("m (u e w) -> m u w e", u=2, e=2),
                     func=ACT.Square,
                     scale=SCALE,
-                    accum_out=z[:, CHUNKS + c : CHUNKS + c + 1],
+                    accum_out=z[:, z0 + CHUNKS + c : z0 + CHUNKS + c + 1],
                 )
 
-        def transpose_and_quantise(h):
-            words = squares[h % SLOTS][:].bitcast(F32)
-            grouped = work.tile([P, CHUNKS * P * PACK], BF16, align_bytes=64, tag="grouped")
+        def transpose_and_quantise(g):
+            words = squares[g][:].bitcast(F32)
+            grouped = work.tile([P, TILES * P * PACK], BF16, align_bytes=64, tag="grouped")
             grouped_words = grouped[:].bitcast(F32)
-            for half in range(2):
-                s2t_ps = psum.tile([P, S], F32, tag="s2t_ps", bufs=3)
-                for n in range(4):
-                    plane = 4 * half + n
+            codes = work.tile([P, TILES * P], U32, align_bytes=64, tag="codes")
+            scales = work.tile([P, TILES * P], U8, align_bytes=64, tag="scales")
+            for bank, copy in enumerate((nc.vector.tensor_copy, nc.scalar.copy, nc.vector.tensor_copy)):
+                tiles = min(2, TILES - 2 * bank)
+                s2t_ps = psum.tile([P, S], F32, tag="s2t_ps", bufs=2)
+                for n in range(2 * tiles):
+                    plane = 4 * bank + n
                     nc.tensor.transpose(
                         s2t_ps[:, n * P : (n + 1) * P], words[:, plane * P : (plane + 1) * P], ident_f32[:]
                     )
-                copy = nc.vector.tensor_copy if half == 0 else nc.scalar.copy
                 copy(
-                    out=grouped_words[:, half * S : (half + 1) * S].rearrange("p (c m u) -> p c m u", c=2, u=2),
-                    in_=s2t_ps[:].rearrange("p (c u m) -> p c m u", c=2, u=2),
+                    out=grouped_words[:, bank * S : bank * S + tiles * 2 * P].rearrange(
+                        "p (t m u) -> p t m u", t=tiles, u=2
+                    ),
+                    in_=s2t_ps[:, 0 : tiles * 2 * P].rearrange("p (t u m) -> p t m u", t=tiles, u=2),
                 )
-            codes = work.tile([P, S], U32, align_bytes=64, tag="codes")
-            scales = work.tile([P, S], U8, align_bytes=64, tag="scales")
-            nc.vector.quantize_mx(out=codes[:].bitcast(FP8X4), scales=scales[:], in_=grouped[:])
-            quantised[h] = (codes, scales)
+            for lo, hi in ((0, 4), (4, TILES)):
+                nc.vector.quantize_mx(
+                    out=codes[:, lo * P : hi * P].bitcast(FP8X4),
+                    scales=scales[:, lo * P : hi * P],
+                    in_=grouped[:, lo * P * PACK : hi * P * PACK],
+                )
+            quantised[g] = (codes, scales)
 
-        def weighted_values(h):
-            codes, scales = quantised[h]
-            z = row_sums[h % SLOTS]
-            o_ps = psum.tile([P, S], F32, tag="o_ps")
-            v_cols = slice(h * D, (h + 1) * D)
-            for c in range(CHUNKS):
-                m_cols = slice(c * P, (c + 1) * P)
-                nc.tensor.matmul_mx(
-                    out=o_ps[:, m_cols],
-                    lhsT=codes[:, m_cols].bitcast(FP8X4),
-                    lhsT_scale=scales[:, m_cols],
-                    rhs=v_codes[:, v_cols].bitcast(FP8X4),
-                    rhs_scale=v_scales[:, v_cols],
-                    start=True,
-                    stop=True,
-                )
-            denom = work.tile([P, CHUNKS], F32, tag="denom")
+        def weighted_values(g):
+            codes, scales = quantised[g]
+            z = row_sums[g % PAIR_SLOTS][:].rearrange("m (a s c) -> m a s c", a=2, s=2)
+            denom = work.tile([P, 2, CHUNKS], F32, tag="denom")
             nc.vector.scalar_tensor_tensor(
                 out=denom[:],
-                in0=z[:, 0:CHUNKS],
+                in0=z[:, :, 0, :],
                 scalar=EPS,
-                in1=z[:, CHUNKS : 2 * CHUNKS],
+                in1=z[:, :, 1, :],
                 op0=ALU.add,
                 op1=ALU.add,
             )
-            inverse = work.tile([P, CHUNKS], F32, tag="inverse")
+            inverse = work.tile([P, 2, CHUNKS], F32, tag="inverse")
             nc.vector.reciprocal(out=inverse[:], in_=denom[:])
-            o_sb = work.tile([P, CHUNKS, D], F32, tag="o_sb", bufs=8)
-            for c in range(CHUNKS):
-                nc.scalar.activation(
-                    out=o_sb[:, c, :],
-                    in_=o_ps[:, c * P : (c + 1) * P],
-                    func=ACT.Copy,
-                    scale=inverse[:, c : c + 1],
-                )
-            nc.sync.dma_start(out=out_rows[:, h, :, :], in_=o_sb[:])
+            for parity in range(2):
+                h = 2 * g + parity
+                o_ps = psum.tile([P, S], F32, tag="o_ps", bufs=2)
+                v_cols = slice(h * D, (h + 1) * D)
+                for c in sorted(range(CHUNKS), key=lambda c: tile_of(h, c)):
+                    t_cols = slice(tile_of(h, c) * P, (tile_of(h, c) + 1) * P)
+                    if c == LAST:
+                        rhs = v_codes[:, v_cols]
+                    else:
+                        first_col = ((h % V_SLOTS) * LAST + c) * D
+                        rhs = masked_v[:, first_col : first_col + D]
+                    nc.tensor.matmul_mx(
+                        out=o_ps[:, c * P : (c + 1) * P],
+                        lhsT=codes[:, t_cols].bitcast(FP8X4),
+                        lhsT_scale=scales[:, t_cols],
+                        rhs=rhs.bitcast(FP8X4),
+                        rhs_scale=v_scales[:, v_cols],
+                        start=True,
+                        stop=True,
+                    )
+                o_sb = work.tile([P, CHUNKS, D], F32, tag="o_sb", bufs=8)
+                for c in range(CHUNKS):
+                    nc.scalar.activation(
+                        out=o_sb[:, c, :],
+                        in_=o_ps[:, c * P : (c + 1) * P],
+                        func=ACT.Copy,
+                        scale=inverse[:, parity, c : c + 1],
+                    )
+                nc.sync.dma_start(out=out_rows[:, h, :, :], in_=o_sb[:])
 
         for step in range(HEADS + 3):
             if step < HEADS:
@@ -232,7 +308,7 @@ def tile_modelnew_t_kernel(tc, q, k, v, out):
                 scores_and_squares(step - 1)
                 if step - 1 in v_group:
                     quantise_v(step - 1)
-            if 0 <= step - 2 < HEADS:
-                transpose_and_quantise(step - 2)
-            if 0 <= step - 3 < HEADS:
-                weighted_values(step - 3)
+            if 0 <= step - 2 < HEADS and (step - 2) % 2 == 1:
+                transpose_and_quantise((step - 2) // 2)
+            if 0 <= step - 3 < HEADS and (step - 3) % 2 == 1:
+                weighted_values((step - 3) // 2)

@@ -6,6 +6,7 @@ from concourse.masks import make_identity
 F32 = mybir.dt.float32
 BF16 = mybir.dt.bfloat16
 U32 = mybir.dt.uint32
+I32 = mybir.dt.int32
 U8 = mybir.dt.uint8
 FP8X4 = mybir.dt.float8_e4m3fn_x4
 ACT = mybir.ActivationFunctionType
@@ -20,6 +21,7 @@ QUARTER = P // PACK
 TILES = 5
 LAST = CHUNKS - 1
 GROUP = 4
+BATCH = 4
 PAIR_SLOTS = 4
 V_SLOTS = 8
 EPS = 1e-6
@@ -55,18 +57,12 @@ def tile_of(h, c):
 def tile_modelnew_t_kernel(tc, q, k, v, out):
     nc = tc.nc
     q_rows = q.rearrange("b h (c m) d -> m (b h c) d", m=P)
+    k_rows = k.rearrange("b h (p j) d -> p (b h) (j d)", j=PACK)
+    v_rows = v.rearrange("b h (p j) d -> p (b h) (j d)", j=PACK)
+    v_groups = [
+        v[:, :, g * P : (g + 1) * P, :].rearrange("b h (r j) d -> r (b h) (j d)", j=PACK) for g in range(CHUNKS)
+    ]
     out_rows = out.rearrange("b h (c m) d -> m (b h) c d", m=P)
-
-    def by_partition(x):
-        return x.rearrange("b h (p j) d -> p (b h) (j d)", j=PACK)
-
-    def by_group(x):
-        return [
-            x[:, :, g * P : (g + 1) * P, :].rearrange("b h (r j) d -> r (b h) (j d)", j=PACK) for g in range(CHUNKS)
-        ]
-
-    k_rows, v_rows = by_partition(k), by_partition(v)
-    k_groups, v_groups = by_group(k), by_group(v)
 
     with ExitStack() as ctx:
         const = ctx.enter_context(tc.tile_pool(name="const", bufs=1))
@@ -96,30 +92,41 @@ def tile_modelnew_t_kernel(tc, q, k, v, out):
             in_=causal[:].rearrange("m (w j) -> m j w", j=PACK),
         )
 
-        def load_keys(dst, rows, groups, first, n):
-            nc.sync.dma_start(out=dst[:, 0:n:2, :], in_=rows[:, first : first + n : 2, :])
-            for g in range(CHUNKS):
-                lo, hi = diag_rows(1, g)
-                nc.sync.dma_start(out=dst[lo:hi, 1:n:2, :], in_=groups[g][:, first + 1 : first + n : 2, :])
+        q_sb, k_sb, v_sb = {}, {}, {}
 
-        groups_of_heads = []
-        loaded = 0
-        while loaded < HEADS:
-            groups_of_heads.append((loaded, min(GROUP, max(2, loaded))))
-            loaded += groups_of_heads[-1][1]
-        q_sb, k_sb = {}, {}
-        v_group = {}
-        for first, n in groups_of_heads:
+        def load_q_k(first, n):
             q_g = loads.tile([P, n * CHUNKS, D], BF16, name="q_g%d" % first)
             nc.sync.dma_start(out=q_g[:], in_=q_rows[:, first * CHUNKS : (first + n) * CHUNKS, :])
             k_g = loads.tile([P, n, PACK * D], BF16, name="k_g%d" % first)
-            load_keys(k_g, k_rows, k_groups, first, n)
-            v_g = loads.tile([P, n, PACK * D], BF16, name="v_g%d" % first)
-            load_keys(v_g, v_rows, v_groups, first, n)
-            v_group[first] = (v_g, n)
+            nc.sync.dma_start(out=k_g[:], in_=k_rows[:, first : first + n, :])
             for i in range(n):
                 q_sb[first + i] = q_g[:, i * CHUNKS : (i + 1) * CHUNKS, :]
                 k_sb[first + i] = k_g[:, i, :]
+
+        def load_v(first, n):
+            half = n // 2
+            even = loads.tile([P, half, PACK * D], BF16, name="v_even%d" % first)
+            nc.sync.dma_start(out=even[:], in_=v_rows[:, first : first + n : 2, :])
+            odd = loads.tile([P, half, PACK * D], BF16, name="v_odd%d" % first)
+            for g in range(CHUNKS):
+                lo, hi = diag_rows(1, g)
+                nc.sync.dma_start(out=odd[lo:hi, :, :], in_=v_groups[g][:, first + 1 : first + n : 2, :])
+            for i in range(0, half, BATCH // 2):
+                v_sb[first + 2 * i] = (even[:, i : i + BATCH // 2, :], odd[:, i : i + BATCH // 2, :])
+
+        load_q_k(0, 1)
+        load_q_k(1, 1)
+        load_q_k(2, 2)
+        load_v(0, 4)
+        load_q_k(4, 4)
+        load_v(4, 4)
+        load_q_k(8, 4)
+        load_v(8, 8)
+        load_q_k(12, 4)
+        load_q_k(16, 4)
+        load_v(16, 16)
+        for first in range(20, HEADS, GROUP):
+            load_q_k(first, GROUP)
 
         v_codes = keep.tile([P, HEADS * D], U32, align_bytes=64)
         v_scales = keep.tile([P, HEADS * D], U8, align_bytes=64)
@@ -136,10 +143,13 @@ def tile_modelnew_t_kernel(tc, q, k, v, out):
         quantised = {}
 
         def quantise_v(first):
-            v_g, n = v_group[first]
-            grouped_v = work.tile([P, n, D, PACK], BF16, align_bytes=64, tag="grouped_v", bufs=2)
-            nc.vector.tensor_copy(out=grouped_v[:], in_=v_g[:].rearrange("p g (j d) -> p g d j", j=PACK))
-            cols = slice(first * D, (first + n) * D)
+            grouped_v = work.tile([P, BATCH, D, PACK], BF16, align_bytes=64, tag="grouped_v", bufs=2)
+            for parity in range(2):
+                nc.vector.tensor_copy(
+                    out=grouped_v[:, parity:BATCH:2, :, :],
+                    in_=v_sb[first][parity].rearrange("p g (j d) -> p g d j", j=PACK),
+                )
+            cols = slice(first * D, (first + BATCH) * D)
             nc.vector.quantize_mx(
                 out=v_codes[:, cols].bitcast(FP8X4),
                 scales=v_scales[:, cols],
@@ -153,9 +163,9 @@ def tile_modelnew_t_kernel(tc, q, k, v, out):
                     lo, hi = seen_rows(parity, c)
                     pieces = [(lo, hi)] if lo != QUARTER else [(lo, 2 * QUARTER), (2 * QUARTER, hi)]
                     for a, b in pieces:
-                        nc.gpsimd.tensor_copy(
-                            out=by_slot[a:b, slot + parity : slot + n : 2, c, :],
-                            in_=by_head[a:b, first + parity : first + n : 2, :],
+                        nc.vector.tensor_copy(
+                            out=by_slot[a:b, slot + parity : slot + BATCH : 2, c, :].bitcast(I32),
+                            in_=by_head[a:b, first + parity : first + BATCH : 2, :].bitcast(I32),
                         )
 
         def transpose_q_k(h):
@@ -184,25 +194,25 @@ def tile_modelnew_t_kernel(tc, q, k, v, out):
             past_b = psum.tile([P, 2 * P], F32, tag="past_b")
             past = {1: past_a[:, 0:P], 3: past_a[:, P : 4 * P], 2: past_b[:, 0 : 2 * P]}
             for c in range(CHUNKS):
-                q_t = qk_t[:, c * P : (c + 1) * P]
-                lo, hi = diag_rows(h, c)
                 nc.tensor.matmul(
                     out=diag_ps[:, c * P : (c + 1) * P].rearrange("m (j w) -> m j w", j=PACK),
-                    lhsT=q_t,
-                    rhs=k_t[:, :, lo:hi],
+                    lhsT=qk_t[:, c * P : (c + 1) * P],
+                    rhs=k_t[:, :, c * QUARTER : (c + 1) * QUARTER],
                     start=True,
                     stop=True,
                 )
             for c in (1, 3, 2):
-                q_t = qk_t[:, c * P : (c + 1) * P]
-                lo, hi = past_rows(h, c)
-                nc.tensor.matmul(
-                    out=past[c].rearrange("m (j w) -> m j w", j=PACK),
-                    lhsT=q_t,
-                    rhs=k_t[:, :, lo:hi],
-                    start=True,
-                    stop=True,
-                )
+                runs = [(0, c, 0)] if h % 2 == 0 else [(g, g + 1, c - 1 - g) for g in range(c)]
+                for g0, g1, place in runs:
+                    nc.tensor.matmul(
+                        out=past[c].rearrange("m (j w) -> m j w", j=PACK)[
+                            :, :, place * QUARTER : (place + g1 - g0) * QUARTER
+                        ],
+                        lhsT=qk_t[:, c * P : (c + 1) * P],
+                        rhs=k_t[:, :, g0 * QUARTER : g1 * QUARTER],
+                        start=True,
+                        stop=True,
+                    )
             masked = work.tile([P, S], F32, tag="masked")
             nc.vector.tensor_tensor(
                 out=masked[:].rearrange("m (c x) -> m c x", c=CHUNKS),
@@ -291,7 +301,7 @@ def tile_modelnew_t_kernel(tc, q, k, v, out):
                         start=True,
                         stop=True,
                     )
-                o_sb = work.tile([P, CHUNKS, D], F32, tag="o_sb", bufs=8)
+                o_sb = work.tile([P, CHUNKS, D], F32, tag="o_sb", bufs=12)
                 for c in range(CHUNKS):
                     nc.scalar.activation(
                         out=o_sb[:, c, :],
@@ -306,7 +316,7 @@ def tile_modelnew_t_kernel(tc, q, k, v, out):
                 transpose_q_k(step)
             if 0 <= step - 1 < HEADS:
                 scores_and_squares(step - 1)
-                if step - 1 in v_group:
+                if (step - 1) % BATCH == 0:
                     quantise_v(step - 1)
             if 0 <= step - 2 < HEADS and (step - 2) % 2 == 1:
                 transpose_and_quantise((step - 2) // 2)

@@ -14,6 +14,7 @@ ALU = mybir.AluOpType
 
 B, H, S, D = 4, 8, 512, 128
 HEADS = B * H
+PAIRS = HEADS // 2
 P = 128
 CHUNKS = 4
 PACK = 4
@@ -92,6 +93,18 @@ def tile_modelnew_t_kernel(tc, q, k, v, out):
             in_=causal[:].rearrange("m (w j) -> m j w", j=PACK),
         )
 
+        v_codes = keep.tile([P, HEADS * D], U32, align_bytes=64)
+        v_scales = keep.tile([P, HEADS * D], U8, align_bytes=64)
+        masked_v = keep.tile([P, V_SLOTS * LAST * D], U32, align_bytes=64)
+        nc.gpsimd.memset(masked_v[:].bitcast(F32), 0.0)
+        row_sums = []
+        for slot in range(PAIR_SLOTS):
+            z = keep.tile([P, 2 * 2 * CHUNKS], F32, name="z_%d" % slot)
+            nc.vector.memset(z[:], 0.0)
+            row_sums.append(z)
+
+        ctx.enter_context(tc.manual_schedule())
+
         q_sb, k_sb, v_sb = {}, {}, {}
 
         def load_q_k(first, n):
@@ -104,69 +117,42 @@ def tile_modelnew_t_kernel(tc, q, k, v, out):
                 k_sb[first + i] = k_g[:, i, :]
 
         def load_v(first, n):
-            half = n // 2
-            even = loads.tile([P, half, PACK * D], BF16, name="v_even%d" % first)
-            nc.sync.dma_start(out=even[:], in_=v_rows[:, first : first + n : 2, :])
-            odd = loads.tile([P, half, PACK * D], BF16, name="v_odd%d" % first)
+            v_g = loads.tile([P, n, PACK * D], BF16, name="v_g%d" % first)
+            nc.sync.dma_start(out=v_g[:, 0:n:2, :], in_=v_rows[:, first : first + n : 2, :])
             for g in range(CHUNKS):
                 lo, hi = diag_rows(1, g)
-                nc.sync.dma_start(out=odd[lo:hi, :, :], in_=v_groups[g][:, first + 1 : first + n : 2, :])
-            for i in range(0, half, BATCH // 2):
-                v_sb[first + 2 * i] = (even[:, i : i + BATCH // 2, :], odd[:, i : i + BATCH // 2, :])
+                nc.sync.dma_start(out=v_g[lo:hi, 1:n:2, :], in_=v_groups[g][:, first + 1 : first + n : 2, :])
+            for i in range(0, n, 2):
+                v_sb[(first + i) // 2] = v_g[:, i : i + 2, :]
 
-        load_q_k(0, 1)
-        load_q_k(1, 1)
-        load_q_k(2, 2)
-        load_v(0, 4)
-        load_q_k(4, 4)
-        load_v(4, 4)
-        load_q_k(8, 4)
-        load_v(8, 8)
-        load_q_k(12, 4)
-        load_q_k(16, 4)
-        load_v(16, 16)
-        for first in range(20, HEADS, GROUP):
-            load_q_k(first, GROUP)
+        turned, transposed, banks, diagonal = {}, {}, {}, {}
+        squares, turned_squares, grouped_squares, quantised = {}, {}, {}, {}
+        grouped_values, inverses, products = {}, {}, {}
 
-        v_codes = keep.tile([P, HEADS * D], U32, align_bytes=64)
-        v_scales = keep.tile([P, HEADS * D], U8, align_bytes=64)
-        masked_v = keep.tile([P, V_SLOTS * LAST * D], U32, align_bytes=64)
-        nc.gpsimd.memset(masked_v[:].bitcast(F32), 0.0)
-        row_sums = []
-        for slot in range(PAIR_SLOTS):
-            z = keep.tile([P, 2 * 2 * CHUNKS], F32, name="z_%d" % slot)
-            nc.vector.memset(z[:], 0.0)
-            row_sums.append(z)
+        def group_v(pair):
+            grouped_v = work.tile([P, 2, D, PACK], BF16, align_bytes=64, tag="grouped_v", bufs=3)
+            nc.vector.tensor_copy(out=grouped_v[:], in_=v_sb[pair].rearrange("p g (j d) -> p g d j", j=PACK))
+            grouped_values[pair] = grouped_v
 
-        transposed = {}
-        squares = {}
-        quantised = {}
-
-        def quantise_v(first):
-            grouped_v = work.tile([P, BATCH, D, PACK], BF16, align_bytes=64, tag="grouped_v", bufs=2)
-            for parity in range(2):
-                nc.vector.tensor_copy(
-                    out=grouped_v[:, parity:BATCH:2, :, :],
-                    in_=v_sb[first][parity].rearrange("p g (j d) -> p g d j", j=PACK),
-                )
-            cols = slice(first * D, (first + BATCH) * D)
+        def quantise_v(pair):
+            cols = slice(2 * pair * D, (2 * pair + 2) * D)
             nc.vector.quantize_mx(
                 out=v_codes[:, cols].bitcast(FP8X4),
                 scales=v_scales[:, cols],
-                in_=grouped_v[:].rearrange("p g d j -> p (g d j)"),
+                in_=grouped_values[pair][:].rearrange("p g d j -> p (g d j)"),
             )
+
+        def mask_v(first):
             by_head = v_codes[:].rearrange("p (h d) -> p h d", d=D)
             by_slot = masked_v[:].rearrange("p (s c d) -> p s c d", c=LAST, d=D)
             slot = first % V_SLOTS
             for c in range(LAST):
                 for parity in range(2):
                     lo, hi = seen_rows(parity, c)
-                    pieces = [(lo, hi)] if lo != QUARTER else [(lo, 2 * QUARTER), (2 * QUARTER, hi)]
-                    for a, b in pieces:
-                        nc.vector.tensor_copy(
-                            out=by_slot[a:b, slot + parity : slot + BATCH : 2, c, :].bitcast(I32),
-                            in_=by_head[a:b, first + parity : first + BATCH : 2, :].bitcast(I32),
-                        )
+                    nc.sync.dma_start(
+                        out=by_slot[lo:hi, slot + parity : slot + BATCH : 2, c, :].bitcast(I32),
+                        in_=by_head[lo:hi, first + parity : first + BATCH : 2, :].bitcast(I32),
+                    )
 
         def transpose_q_k(h):
             qk_ps = psum.tile([P, 2 * S], BF16, tag="qk_ps")
@@ -176,19 +162,16 @@ def tile_modelnew_t_kernel(tc, q, k, v, out):
                 nc.tensor.transpose(
                     qk_ps[:, S + j * P : S + (j + 1) * P], k_sb[h][:, j * D : (j + 1) * D], ident_bf[:]
                 )
+            turned[h] = qk_ps
+
+        def copy_q_k(h):
             qk_t = work.tile([P, 2 * S], BF16, tag="qk_t")
-            nc.vector.tensor_copy(out=qk_t[:], in_=qk_ps[:])
+            nc.vector.tensor_copy(out=qk_t[:], in_=turned[h][:])
             transposed[h] = qk_t
 
-        def scores_and_squares(h):
+        def scores(h):
             qk_t = transposed[h]
             k_t = qk_t[:, S : 2 * S].rearrange("d (j p) -> d j p", j=PACK)
-            if h % 2 == 0:
-                s2_new = work.tile([P, TILES * 2 * 2 * P], BF16, tag="s2")
-                squares[h // 2] = s2_new
-            s2 = squares[h // 2][:].rearrange("m (t u x) -> m t u x", t=TILES, u=2)
-            z = row_sums[(h // 2) % PAIR_SLOTS]
-            z0 = (h % 2) * 2 * CHUNKS
             diag_ps = psum.tile([P, S], F32, tag="diag_ps")
             past_a = psum.tile([P, S], F32, tag="past_a")
             past_b = psum.tile([P, 2 * P], F32, tag="past_b")
@@ -213,13 +196,27 @@ def tile_modelnew_t_kernel(tc, q, k, v, out):
                         start=True,
                         stop=True,
                     )
+            banks[h] = (diag_ps, past)
+
+        def mask(h):
             masked = work.tile([P, S], F32, tag="masked")
             nc.vector.tensor_tensor(
                 out=masked[:].rearrange("m (c x) -> m c x", c=CHUNKS),
-                in0=diag_ps[:].rearrange("m (c x) -> m c x", c=CHUNKS),
+                in0=banks[h][0][:].rearrange("m (c x) -> m c x", c=CHUNKS),
                 in1=causal_jw[:].unsqueeze(1).to_broadcast([P, CHUNKS, P]),
                 op=ALU.mult,
             )
+            diagonal[h] = masked
+
+        def square(h):
+            if h % 2 == 0:
+                s2_new = work.tile([P, TILES * 2 * 2 * P], BF16, tag="s2")
+                squares[h // 2] = s2_new
+            s2 = squares[h // 2][:].rearrange("m (t u x) -> m t u x", t=TILES, u=2)
+            z = row_sums[(h // 2) % PAIR_SLOTS]
+            z0 = (h % 2) * 2 * CHUNKS
+            past = banks[h][1]
+            masked = diagonal[h]
             for c in (1, 3, 2):
                 lo, hi = past_rows(h, c)
                 nc.scalar.activation(
@@ -239,36 +236,42 @@ def tile_modelnew_t_kernel(tc, q, k, v, out):
                     accum_out=z[:, z0 + CHUNKS + c : z0 + CHUNKS + c + 1],
                 )
 
-        def transpose_and_quantise(g):
+        def transpose_squares(g):
             words = squares[g][:].bitcast(F32)
-            grouped = work.tile([P, TILES * P * PACK], BF16, align_bytes=64, tag="grouped")
-            grouped_words = grouped[:].bitcast(F32)
-            codes = work.tile([P, TILES * P], U32, align_bytes=64, tag="codes")
-            scales = work.tile([P, TILES * P], U8, align_bytes=64, tag="scales")
-            for bank, copy in enumerate((nc.vector.tensor_copy, nc.scalar.copy, nc.vector.tensor_copy)):
+            turned_squares[g] = {}
+            for bank in (2, 0, 1):
                 tiles = min(2, TILES - 2 * bank)
-                s2t_ps = psum.tile([P, S], F32, tag="s2t_ps", bufs=2)
+                s2t_ps = psum.tile([P, S], F32, tag="ring", bufs=4)
                 for n in range(2 * tiles):
                     plane = 4 * bank + n
                     nc.tensor.transpose(
                         s2t_ps[:, n * P : (n + 1) * P], words[:, plane * P : (plane + 1) * P], ident_f32[:]
                     )
-                copy(
-                    out=grouped_words[:, bank * S : bank * S + tiles * 2 * P].rearrange(
-                        "p (t m u) -> p t m u", t=tiles, u=2
-                    ),
-                    in_=s2t_ps[:, 0 : tiles * 2 * P].rearrange("p (t u m) -> p t m u", t=tiles, u=2),
-                )
+                turned_squares[g][bank] = s2t_ps
+            grouped = work.tile([P, TILES * P * PACK], BF16, align_bytes=64, tag="grouped")
+            grouped_squares[g] = grouped
+
+        def copy_squares(g, bank, copy):
+            tiles = min(2, TILES - 2 * bank)
+            copy(
+                out=grouped_squares[g][:]
+                .bitcast(F32)[:, bank * S : bank * S + tiles * 2 * P]
+                .rearrange("p (t m u) -> p t m u", t=tiles, u=2),
+                in_=turned_squares[g][bank][:, 0 : tiles * 2 * P].rearrange("p (t u m) -> p t m u", t=tiles, u=2),
+            )
+
+        def quantise(g):
+            codes = work.tile([P, TILES * P], U32, align_bytes=64, tag="codes")
+            scales = work.tile([P, TILES * P], U8, align_bytes=64, tag="scales")
             for lo, hi in ((0, 4), (4, TILES)):
                 nc.vector.quantize_mx(
                     out=codes[:, lo * P : hi * P].bitcast(FP8X4),
                     scales=scales[:, lo * P : hi * P],
-                    in_=grouped[:, lo * P * PACK : hi * P * PACK],
+                    in_=grouped_squares[g][:, lo * P * PACK : hi * P * PACK],
                 )
             quantised[g] = (codes, scales)
 
-        def weighted_values(g):
-            codes, scales = quantised[g]
+        def denominators(g):
             z = row_sums[g % PAIR_SLOTS][:].rearrange("m (a s c) -> m a s c", a=2, s=2)
             denom = work.tile([P, 2, CHUNKS], F32, tag="denom")
             nc.vector.scalar_tensor_tensor(
@@ -279,11 +282,15 @@ def tile_modelnew_t_kernel(tc, q, k, v, out):
                 op0=ALU.add,
                 op1=ALU.add,
             )
-            inverse = work.tile([P, 2, CHUNKS], F32, tag="inverse")
+            inverse = work.tile([P, 2, CHUNKS], F32, tag="inverse", bufs=4)
             nc.vector.reciprocal(out=inverse[:], in_=denom[:])
+            inverses[g] = inverse
+
+        def weighted_values(g):
+            codes, scales = quantised[g]
             for parity in range(2):
                 h = 2 * g + parity
-                o_ps = psum.tile([P, S], F32, tag="o_ps", bufs=2)
+                o_ps = psum.tile([P, S], F32, tag="ring", bufs=4)
                 v_cols = slice(h * D, (h + 1) * D)
                 for c in sorted(range(CHUNKS), key=lambda c: tile_of(h, c)):
                     t_cols = slice(tile_of(h, c) * P, (tile_of(h, c) + 1) * P)
@@ -301,24 +308,80 @@ def tile_modelnew_t_kernel(tc, q, k, v, out):
                         start=True,
                         stop=True,
                     )
-                o_sb = work.tile([P, CHUNKS, D], F32, tag="o_sb", bufs=12)
+                products[h] = o_ps
+
+        def scale_and_store(h, on_vector):
+            o_ps = products[h]
+            inverse = inverses[h // 2]
+            o_sb = work.tile([P, CHUNKS, D], F32, tag="o_sb", bufs=8)
+            if on_vector:
+                nc.vector.tensor_tensor(
+                    out=o_sb[:],
+                    in0=o_ps[:].rearrange("m (c d) -> m c d", c=CHUNKS),
+                    in1=inverse[:, h % 2, :].unsqueeze(2).to_broadcast([P, CHUNKS, D]),
+                    op=ALU.mult,
+                )
+            else:
                 for c in range(CHUNKS):
                     nc.scalar.activation(
                         out=o_sb[:, c, :],
                         in_=o_ps[:, c * P : (c + 1) * P],
                         func=ACT.Copy,
-                        scale=inverse[:, parity, c : c + 1],
+                        scale=inverse[:, h % 2, c : c + 1],
                     )
-                nc.sync.dma_start(out=out_rows[:, h, :, :], in_=o_sb[:])
+            nc.sync.dma_start(out=out_rows[:, h, :, :], in_=o_sb[:])
 
-        for step in range(HEADS + 3):
-            if step < HEADS:
-                transpose_q_k(step)
-            if 0 <= step - 1 < HEADS:
-                scores_and_squares(step - 1)
-                if (step - 1) % BATCH == 0:
-                    quantise_v(step - 1)
-            if 0 <= step - 2 < HEADS and (step - 2) % 2 == 1:
-                transpose_and_quantise((step - 2) // 2)
-            if 0 <= step - 3 < HEADS and (step - 3) % 2 == 1:
-                weighted_values((step - 3) // 2)
+        load_q_k(0, 1)
+        load_q_k(1, 1)
+        load_q_k(2, 2)
+        load_v(0, 4)
+        load_q_k(4, 4)
+        load_v(4, 4)
+        load_q_k(8, 4)
+
+        for step in range(-2, HEADS + 4):
+            if step == 0:
+                load_v(8, 8)
+            if step == 6:
+                load_v(16, 16)
+            if 12 <= step + 10 < HEADS and (step + 10) % GROUP == 0:
+                load_q_k(step + 10, GROUP)
+            if 0 <= step < HEADS:
+                scores(step)
+                mask(step)
+                square(step)
+            if 0 <= step + 1 < HEADS:
+                copy_q_k(step + 1)
+            if step % 2 == 0:
+                g = (step - 2) // 2
+                live = 0 <= g < PAIRS
+                if live:
+                    transpose_squares(g)
+                if 0 <= step + 2 < HEADS:
+                    transpose_q_k(step + 2)
+                if live:
+                    copy_squares(g, 0, nc.scalar.copy)
+                    copy_squares(g, 1, nc.scalar.copy)
+                pairs = [0, 1] if step == 0 else [(step + 2) // 2]
+                pairs = [pair for pair in pairs if step >= 0 and pair < PAIRS]
+                for pair in pairs:
+                    group_v(pair)
+                if live:
+                    copy_squares(g, 2, nc.vector.tensor_copy)
+                    denominators(g)
+                for pair in pairs:
+                    quantise_v(pair)
+                    if pair % 2 == 1:
+                        mask_v(2 * (pair - 1))
+            else:
+                g = (step - 5) // 2
+                live = 0 <= g < PAIRS
+                if live:
+                    weighted_values(g)
+                if 0 <= step + 2 < HEADS:
+                    transpose_q_k(step + 2)
+                if live:
+                    scale_and_store(2 * g + 1, False)
+                    scale_and_store(2 * g, True)
+                if 0 <= (step - 3) // 2 < PAIRS:
+                    quantise((step - 3) // 2)

@@ -24,6 +24,7 @@ LAST = CHUNKS - 1
 GROUP = 4
 BATCH = 4
 PAIR_SLOTS = 4
+V_PIECES = 1
 V_SLOTS = 8
 EPS = 1e-6
 SCALE = D ** -0.5
@@ -103,6 +104,9 @@ def tile_modelnew_t_kernel(tc, q, k, v, out):
             nc.vector.memset(z[:], 0.0)
             row_sums.append(z)
 
+        minus_one = const.tile([P, 2, CHUNKS], F32)
+        nc.gpsimd.memset(minus_one[:], -1.0)
+
         ctx.enter_context(tc.manual_schedule())
 
         q_sb, k_sb, v_sb = {}, {}, {}
@@ -130,8 +134,18 @@ def tile_modelnew_t_kernel(tc, q, k, v, out):
         grouped_values, inverses, products = {}, {}, {}
 
         def group_v(pair):
-            grouped_v = work.tile([P, 2, D, PACK], BF16, align_bytes=64, tag="grouped_v", bufs=3)
-            nc.vector.tensor_copy(out=grouped_v[:], in_=v_sb[pair].rearrange("p g (j d) -> p g d j", j=PACK))
+            grouped_v = work.tile([P, 2, D, PACK], BF16, align_bytes=64, tag="grouped_v", bufs=1)
+            by_column = v_sb[pair].rearrange("p g (j d) -> p g d j", j=PACK)
+            for i in range(2):
+                for d0 in range(0, D, D // V_PIECES):
+                    nc.gpsimd.tensor_scalar(
+                        out=grouped_v[:, i, d0 : d0 + D // V_PIECES, :],
+                        in0=by_column[:, i, d0 : d0 + D // V_PIECES, :],
+                        scalar1=1.0,
+                        scalar2=0.0,
+                        op0=ALU.mult,
+                        op1=ALU.add,
+                    )
             grouped_values[pair] = grouped_v
 
         def quantise_v(pair):
@@ -273,17 +287,12 @@ def tile_modelnew_t_kernel(tc, q, k, v, out):
 
         def denominators(g):
             z = row_sums[g % PAIR_SLOTS][:].rearrange("m (a s c) -> m a s c", a=2, s=2)
+            total = work.tile([P, 2, CHUNKS], F32, tag="total")
+            nc.gpsimd.tensor_tensor(out=total[:], in0=z[:, :, 0, :], in1=z[:, :, 1, :], op=ALU.add)
             denom = work.tile([P, 2, CHUNKS], F32, tag="denom")
-            nc.vector.scalar_tensor_tensor(
-                out=denom[:],
-                in0=z[:, :, 0, :],
-                scalar=EPS,
-                in1=z[:, :, 1, :],
-                op0=ALU.add,
-                op1=ALU.add,
-            )
+            nc.gpsimd.tensor_scalar(out=denom[:], in0=total[:], scalar1=EPS, scalar2=1.0, op0=ALU.add, op1=ALU.mult)
             inverse = work.tile([P, 2, CHUNKS], F32, tag="inverse", bufs=4)
-            nc.vector.reciprocal(out=inverse[:], in_=denom[:])
+            nc.gpsimd.tensor_tensor(out=inverse[:], in0=denom[:], in1=minus_one[:], op=ALU.pow)
             inverses[g] = inverse
 
         def weighted_values(g):
@@ -339,6 +348,14 @@ def tile_modelnew_t_kernel(tc, q, k, v, out):
         load_v(4, 4)
         load_q_k(8, 4)
 
+        def next_v(pair):
+            quantise_v(pair)
+            if pair % 2 == 1:
+                mask_v(2 * (pair - 1))
+            if pair + 1 < PAIRS:
+                group_v(pair + 1)
+
+        group_v(0)
         for step in range(-2, HEADS + 4):
             if step == 0:
                 load_v(8, 8)
@@ -361,18 +378,15 @@ def tile_modelnew_t_kernel(tc, q, k, v, out):
                     transpose_q_k(step + 2)
                 if live:
                     copy_squares(g, 0, nc.scalar.copy)
-                    copy_squares(g, 1, nc.scalar.copy)
-                pairs = [0, 1] if step == 0 else [(step + 2) // 2]
-                pairs = [pair for pair in pairs if step >= 0 and pair < PAIRS]
-                for pair in pairs:
-                    group_v(pair)
+                    denominators(g)
+                if 0 <= g - 1 < PAIRS:
+                    quantise(g - 1)
                 if live:
                     copy_squares(g, 2, nc.vector.tensor_copy)
-                    denominators(g)
-                for pair in pairs:
-                    quantise_v(pair)
-                    if pair % 2 == 1:
-                        mask_v(2 * (pair - 1))
+                if step == 0:
+                    next_v(0)
+                if 2 <= (step + 2) // 2 < PAIRS:
+                    next_v((step + 2) // 2)
             else:
                 g = (step - 5) // 2
                 live = 0 <= g < PAIRS
@@ -380,8 +394,10 @@ def tile_modelnew_t_kernel(tc, q, k, v, out):
                     weighted_values(g)
                 if 0 <= step + 2 < HEADS:
                     transpose_q_k(step + 2)
-                if live:
-                    scale_and_store(2 * g + 1, False)
-                    scale_and_store(2 * g, True)
                 if 0 <= (step - 3) // 2 < PAIRS:
-                    quantise((step - 3) // 2)
+                    copy_squares((step - 3) // 2, 1, nc.scalar.copy)
+                if live:
+                    scale_and_store(2 * g, True)
+                    scale_and_store(2 * g + 1, True)
+                if step == 1:
+                    next_v(1)

@@ -32,38 +32,37 @@ SCALE = D ** -0.5
 FLOPS = 2 * (2 * HEADS * S * S * D)
 
 
+def shift_of(h, c):
+    if c == 0:
+        return LAST
+    if c == 1 and h % 2 == 1:
+        return 2
+    return 0
+
+
 def diag_rows(h, c):
-    if h % 2 == 0:
-        return c * QUARTER, (c + 1) * QUARTER
-    return (LAST - c) * QUARTER, (CHUNKS - c) * QUARTER
+    first = (shift_of(h, c) + c) * QUARTER
+    return first, first + QUARTER
 
 
 def past_rows(h, c):
-    if h % 2 == 0:
-        return 0, c * QUARTER
-    return (CHUNKS - c) * QUARTER, P
-
-
-def seen_rows(h, c):
-    if h % 2 == 0:
-        return 0, (c + 1) * QUARTER
-    return (LAST - c) * QUARTER, P
+    first = shift_of(h, c) * QUARTER
+    return first, first + c * QUARTER
 
 
 def tile_of(h, c):
     if c == LAST:
         return h % 2
-    return 2 + (c if h % 2 == 0 else LAST - 1 - c)
+    if c == 1:
+        return 3
+    return 2 if (c == 2) == (h % 2 == 0) else 4
 
 
 def tile_modelnew_t_kernel(tc, q, k, v, out):
     nc = tc.nc
-    q_rows = q.rearrange("b h (c m) d -> m (b h c) d", m=P)
+    q_rows = q.rearrange("b h (p e) d -> p (b h) (e d)", e=PACK)
     k_rows = k.rearrange("b h (p j) d -> p (b h) (j d)", j=PACK)
     v_rows = v.rearrange("b h (p j) d -> p (b h) (j d)", j=PACK)
-    v_groups = [
-        v[:, :, g * P : (g + 1) * P, :].rearrange("b h (r j) d -> r (b h) (j d)", j=PACK) for g in range(CHUNKS)
-    ]
     out_rows = out.rearrange("b h (c m) d -> m (b h) c d", m=P)
 
     with ExitStack() as ctx:
@@ -72,6 +71,20 @@ def tile_modelnew_t_kernel(tc, q, k, v, out):
         keep = ctx.enter_context(tc.tile_pool(name="keep", bufs=1))
         work = ctx.enter_context(tc.tile_pool(name="work", bufs=3))
         psum = ctx.enter_context(tc.psum_pool(name="psum", bufs=1))
+
+        ctx.enter_context(tc.manual_schedule())
+
+        v_codes = keep.tile([P, HEADS * D], U32, align_bytes=64)
+        v_scales = keep.tile([P, HEADS * D], U8, align_bytes=64)
+        masked_v = keep.tile([P, LAST * V_SLOTS * D], U32, align_bytes=64)
+        moved_scales = keep.tile([P, 2 * V_SLOTS * D], U8, align_bytes=64)
+        row_sums = []
+        for slot in range(PAIR_SLOTS):
+            z = keep.tile([P, 2 * 2 * CHUNKS], F32, name="z_%d" % slot)
+            nc.vector.memset(z[:], 0.0)
+            row_sums.append(z)
+        nc.vector.memset(v_scales[:].bitcast(I32), 0)
+        nc.vector.memset(moved_scales[:].bitcast(I32), 0)
 
         ident_bf = const.tile([P, P], BF16)
         make_identity(nc, ident_bf[:])
@@ -88,50 +101,46 @@ def tile_modelnew_t_kernel(tc, q, k, v, out):
             pattern=[[-1, P]],
             channel_multiplier=1,
         )
-        causal_jw = const.tile([P, P], F32)
-        nc.vector.tensor_copy(
-            out=causal_jw[:].rearrange("m (j w) -> m j w", j=PACK),
-            in_=causal[:].rearrange("m (w j) -> m j w", j=PACK),
-        )
-
-        v_codes = keep.tile([P, HEADS * D], U32, align_bytes=64)
-        v_scales = keep.tile([P, HEADS * D], U8, align_bytes=64)
-        masked_v = keep.tile([P, V_SLOTS * LAST * D], U32, align_bytes=64)
-        nc.gpsimd.memset(masked_v[:].bitcast(F32), 0.0)
-        row_sums = []
-        for slot in range(PAIR_SLOTS):
-            z = keep.tile([P, 2 * 2 * CHUNKS], F32, name="z_%d" % slot)
-            nc.vector.memset(z[:], 0.0)
-            row_sums.append(z)
-
         minus_one = const.tile([P, 2, CHUNKS], F32)
         nc.gpsimd.memset(minus_one[:], -1.0)
-
-        ctx.enter_context(tc.manual_schedule())
+        nc.gpsimd.memset(masked_v[:].bitcast(F32), 0.0)
+        to_mixed = const.tile([P, P], F32)
+        nc.vector.tensor_copy(
+            out=to_mixed[:].rearrange("n (e r) -> n e r", e=PACK),
+            in_=ident_f32[:].rearrange("n (r e) -> n e r", e=PACK),
+        )
+        to_plain = const.tile([P, P], F32)
+        nc.vector.tensor_copy(
+            out=to_plain[:].rearrange("m (r e) -> m r e", e=PACK),
+            in_=ident_f32[:].rearrange("m (e r) -> m r e", e=PACK),
+        )
+        causal_plain = const.tile([P, P], F32)
+        nc.vector.tensor_copy(
+            out=causal_plain[:].rearrange("n (j w) -> n j w", j=PACK),
+            in_=causal[:].rearrange("n (w j) -> n j w", j=PACK),
+        )
+        causal_jw = const.tile([P, P], F32)
 
         q_sb, k_sb, v_sb = {}, {}, {}
 
         def load_q_k(first, n):
-            q_g = loads.tile([P, n * CHUNKS, D], BF16, name="q_g%d" % first)
-            nc.sync.dma_start(out=q_g[:], in_=q_rows[:, first * CHUNKS : (first + n) * CHUNKS, :])
+            q_g = loads.tile([P, n, PACK * D], BF16, name="q_g%d" % first)
+            nc.sync.dma_start(out=q_g[:], in_=q_rows[:, first : first + n, :])
             k_g = loads.tile([P, n, PACK * D], BF16, name="k_g%d" % first)
             nc.sync.dma_start(out=k_g[:], in_=k_rows[:, first : first + n, :])
             for i in range(n):
-                q_sb[first + i] = q_g[:, i * CHUNKS : (i + 1) * CHUNKS, :]
+                q_sb[first + i] = q_g[:, i, :]
                 k_sb[first + i] = k_g[:, i, :]
 
         def load_v(first, n):
             v_g = loads.tile([P, n, PACK * D], BF16, name="v_g%d" % first)
-            nc.sync.dma_start(out=v_g[:, 0:n:2, :], in_=v_rows[:, first : first + n : 2, :])
-            for g in range(CHUNKS):
-                lo, hi = diag_rows(1, g)
-                nc.sync.dma_start(out=v_g[lo:hi, 1:n:2, :], in_=v_groups[g][:, first + 1 : first + n : 2, :])
+            nc.sync.dma_start(out=v_g[:], in_=v_rows[:, first : first + n, :])
             for i in range(0, n, 2):
                 v_sb[(first + i) // 2] = v_g[:, i : i + 2, :]
 
         turned, transposed, banks, diagonal = {}, {}, {}, {}
         squares, turned_squares, grouped_squares, quantised = {}, {}, {}, {}
-        grouped_values, inverses, products = {}, {}, {}
+        grouped_values, inverses, products, plain_sums = {}, {}, {}, {}
 
         def group_v(pair):
             grouped_v = work.tile([P, 2, D, PACK], BF16, align_bytes=64, tag="grouped_v", bufs=1)
@@ -157,21 +166,34 @@ def tile_modelnew_t_kernel(tc, q, k, v, out):
             )
 
         def mask_v(first):
-            by_head = v_codes[:].rearrange("p (h d) -> p h d", d=D)
-            by_slot = masked_v[:].rearrange("p (s c d) -> p s c d", c=LAST, d=D)
+            codes_by_head = v_codes[:].rearrange("p (h d) -> p h d", d=D)
+            codes_by_slot = masked_v[:].rearrange("p (c s d) -> p c s d", c=LAST, d=D)
+            scales_by_head = v_scales[:].rearrange("p (h d) -> p h d", d=D)
+            scales_by_slot = moved_scales[:].rearrange("p (c s d) -> p c s d", c=2, d=D)
             slot = first % V_SLOTS
-            for c in range(LAST):
-                for parity in range(2):
-                    lo, hi = seen_rows(parity, c)
+            for c, start, step in ((0, 0, 1), (1, 0, 2), (1, 1, 2), (2, 0, 1)):
+                rows = (c + 1) * QUARTER
+                to = shift_of(start, c) * QUARTER
+                nc.sync.dma_start(
+                    out=codes_by_slot[to : to + rows, c, slot + start : slot + BATCH : step, :].bitcast(I32),
+                    in_=codes_by_head[0:rows, first + start : first + BATCH : step, :].bitcast(I32),
+                )
+                if to > 0:
                     nc.sync.dma_start(
-                        out=by_slot[lo:hi, slot + parity : slot + BATCH : 2, c, :].bitcast(I32),
-                        in_=by_head[lo:hi, first + parity : first + BATCH : 2, :].bitcast(I32),
+                        out=scales_by_slot[to : to + rows, c, slot + start : slot + BATCH : step, :].bitcast(I32),
+                        in_=scales_by_head[0:rows, first + start : first + BATCH : step, :].bitcast(I32),
                     )
+
+        def permute_mask():
+            causal_ps = psum.tile([P, S], F32, tag="past_a")
+            nc.tensor.matmul(out=causal_ps[:, 0:P], lhsT=to_mixed[:], rhs=causal_plain[:], start=True, stop=True)
+            nc.vector.tensor_copy(out=causal_jw[:], in_=causal_ps[:, 0:P])
 
         def transpose_q_k(h):
             qk_ps = psum.tile([P, 2 * S], BF16, tag="qk_ps")
-            for c in range(CHUNKS):
-                nc.tensor.transpose(qk_ps[:, c * P : (c + 1) * P], q_sb[h][:, c, :], ident_bf[:])
+            q_cols = qk_ps[:, 0:S].rearrange("d (c e r) -> d e c r", c=CHUNKS, e=PACK)
+            for e in range(PACK):
+                nc.tensor.transpose(q_cols[:, e, :, :], q_sb[h][:, e * D : (e + 1) * D], ident_bf[:])
             for j in range(PACK):
                 nc.tensor.transpose(
                     qk_ps[:, S + j * P : S + (j + 1) * P], k_sb[h][:, j * D : (j + 1) * D], ident_bf[:]
@@ -199,17 +221,13 @@ def tile_modelnew_t_kernel(tc, q, k, v, out):
                     stop=True,
                 )
             for c in (1, 3, 2):
-                runs = [(0, c, 0)] if h % 2 == 0 else [(g, g + 1, c - 1 - g) for g in range(c)]
-                for g0, g1, place in runs:
-                    nc.tensor.matmul(
-                        out=past[c].rearrange("m (j w) -> m j w", j=PACK)[
-                            :, :, place * QUARTER : (place + g1 - g0) * QUARTER
-                        ],
-                        lhsT=qk_t[:, c * P : (c + 1) * P],
-                        rhs=k_t[:, :, g0 * QUARTER : g1 * QUARTER],
-                        start=True,
-                        stop=True,
-                    )
+                nc.tensor.matmul(
+                    out=past[c].rearrange("m (j w) -> m j w", j=PACK),
+                    lhsT=qk_t[:, c * P : (c + 1) * P],
+                    rhs=k_t[:, :, 0 : c * QUARTER],
+                    start=True,
+                    stop=True,
+                )
             banks[h] = (diag_ps, past)
 
         def mask(h):
@@ -256,10 +274,18 @@ def tile_modelnew_t_kernel(tc, q, k, v, out):
             for bank in (2, 0, 1):
                 tiles = min(2, TILES - 2 * bank)
                 s2t_ps = psum.tile([P, S], F32, tag="ring", bufs=4)
+                if tiles == 1:
+                    nc.tensor.matmul(
+                        out=s2t_ps[:, 2 * P : 2 * P + 4 * CHUNKS],
+                        lhsT=to_plain[:],
+                        rhs=row_sums[g % PAIR_SLOTS][:],
+                        start=True,
+                        stop=True,
+                    )
                 for n in range(2 * tiles):
                     plane = 4 * bank + n
                     nc.tensor.transpose(
-                        s2t_ps[:, n * P : (n + 1) * P], words[:, plane * P : (plane + 1) * P], ident_f32[:]
+                        s2t_ps[:, n * P : (n + 1) * P], words[:, plane * P : (plane + 1) * P], to_plain[:]
                     )
                 turned_squares[g][bank] = s2t_ps
             grouped = work.tile([P, TILES * P * PACK], BF16, align_bytes=64, tag="grouped")
@@ -285,8 +311,13 @@ def tile_modelnew_t_kernel(tc, q, k, v, out):
                 )
             quantised[g] = (codes, scales)
 
+        def copy_sums(g):
+            sums = work.tile([P, 4 * CHUNKS], F32, tag="sums")
+            nc.vector.tensor_copy(out=sums[:], in_=turned_squares[g][2][:, 2 * P : 2 * P + 4 * CHUNKS])
+            plain_sums[g] = sums
+
         def denominators(g):
-            z = row_sums[g % PAIR_SLOTS][:].rearrange("m (a s c) -> m a s c", a=2, s=2)
+            z = plain_sums[g][:].rearrange("m (a s c) -> m a s c", a=2, s=2)
             total = work.tile([P, 2, CHUNKS], F32, tag="total")
             nc.gpsimd.tensor_tensor(out=total[:], in0=z[:, :, 0, :], in1=z[:, :, 1, :], op=ALU.add)
             denom = work.tile([P, 2, CHUNKS], F32, tag="denom")
@@ -303,17 +334,15 @@ def tile_modelnew_t_kernel(tc, q, k, v, out):
                 v_cols = slice(h * D, (h + 1) * D)
                 for c in sorted(range(CHUNKS), key=lambda c: tile_of(h, c)):
                     t_cols = slice(tile_of(h, c) * P, (tile_of(h, c) + 1) * P)
-                    if c == LAST:
-                        rhs = v_codes[:, v_cols]
-                    else:
-                        first_col = ((h % V_SLOTS) * LAST + c) * D
-                        rhs = masked_v[:, first_col : first_col + D]
+                    slot_cols = slice((c * V_SLOTS + h % V_SLOTS) * D, (c * V_SLOTS + h % V_SLOTS + 1) * D)
+                    rhs = v_codes[:, v_cols] if c == LAST else masked_v[:, slot_cols]
+                    rhs_scale = moved_scales[:, slot_cols] if shift_of(h, c) > 0 else v_scales[:, v_cols]
                     nc.tensor.matmul_mx(
                         out=o_ps[:, c * P : (c + 1) * P],
                         lhsT=codes[:, t_cols].bitcast(FP8X4),
                         lhsT_scale=scales[:, t_cols],
                         rhs=rhs.bitcast(FP8X4),
-                        rhs_scale=v_scales[:, v_cols],
+                        rhs_scale=rhs_scale,
                         start=True,
                         stop=True,
                     )
@@ -346,7 +375,6 @@ def tile_modelnew_t_kernel(tc, q, k, v, out):
         load_v(0, 4)
         load_q_k(4, 4)
         load_v(4, 4)
-        load_q_k(8, 4)
 
         def next_v(pair):
             quantise_v(pair)
@@ -357,18 +385,18 @@ def tile_modelnew_t_kernel(tc, q, k, v, out):
 
         group_v(0)
         for step in range(-2, HEADS + 4):
-            if step == 0:
-                load_v(8, 8)
-            if step == 6:
-                load_v(16, 16)
-            if 12 <= step + 10 < HEADS and (step + 10) % GROUP == 0:
-                load_q_k(step + 10, GROUP)
+            if step % GROUP == 3 and step + 9 < HEADS:
+                load_v(step + 9, GROUP)
+            if step % GROUP == 1 and step + 7 < HEADS:
+                load_q_k(step + 7, GROUP)
             if 0 <= step < HEADS:
                 scores(step)
                 mask(step)
                 square(step)
             if 0 <= step + 1 < HEADS:
                 copy_q_k(step + 1)
+            if step == -1:
+                permute_mask()
             if step % 2 == 0:
                 g = (step - 2) // 2
                 live = 0 <= g < PAIRS
@@ -378,15 +406,17 @@ def tile_modelnew_t_kernel(tc, q, k, v, out):
                     transpose_q_k(step + 2)
                 if live:
                     copy_squares(g, 0, nc.scalar.copy)
-                    denominators(g)
-                if 0 <= g - 1 < PAIRS:
-                    quantise(g - 1)
                 if live:
                     copy_squares(g, 2, nc.vector.tensor_copy)
+                    copy_sums(g)
+                if 0 <= g - 1 < PAIRS - 1:
+                    quantise(g - 1)
                 if step == 0:
                     next_v(0)
                 if 2 <= (step + 2) // 2 < PAIRS:
                     next_v((step + 2) // 2)
+                if live:
+                    denominators(g)
             else:
                 g = (step - 5) // 2
                 live = 0 <= g < PAIRS
@@ -398,6 +428,8 @@ def tile_modelnew_t_kernel(tc, q, k, v, out):
                     copy_squares((step - 3) // 2, 1, nc.scalar.copy)
                 if live:
                     scale_and_store(2 * g, True)
-                    scale_and_store(2 * g + 1, True)
+                    if g == PAIRS - 2:
+                        quantise(PAIRS - 1)
+                    scale_and_store(2 * g + 1, g < PAIRS - 1)
                 if step == 1:
                     next_v(1)

@@ -76,15 +76,15 @@ def tile_modelnew_t_kernel(tc, q, k, v, out):
 
         v_codes = keep.tile([P, HEADS * D], U32, align_bytes=64)
         v_scales = keep.tile([P, HEADS * D], U8, align_bytes=64)
-        masked_v = keep.tile([P, LAST * V_SLOTS * D], U32, align_bytes=64)
-        moved_scales = keep.tile([P, 2 * V_SLOTS * D], U8, align_bytes=64)
+        moved_v = keep.tile([P, 2 * V_SLOTS * D], U32, align_bytes=64)
+        chunk_scales = keep.tile([P, LAST * V_SLOTS * D], U8, align_bytes=64)
         row_sums = []
         for slot in range(PAIR_SLOTS):
             z = keep.tile([P, 2 * 2 * CHUNKS], F32, name="z_%d" % slot)
             nc.vector.memset(z[:], 0.0)
             row_sums.append(z)
         nc.vector.memset(v_scales[:].bitcast(I32), 0)
-        nc.vector.memset(moved_scales[:].bitcast(I32), 0)
+        nc.vector.memset(chunk_scales[:].bitcast(I32), 0)
 
         ident_bf = const.tile([P, P], BF16)
         make_identity(nc, ident_bf[:])
@@ -103,7 +103,7 @@ def tile_modelnew_t_kernel(tc, q, k, v, out):
         )
         minus_one = const.tile([P, 2, CHUNKS], F32)
         nc.gpsimd.memset(minus_one[:], -1.0)
-        nc.gpsimd.memset(masked_v[:].bitcast(F32), 0.0)
+        nc.gpsimd.memset(moved_v[:].bitcast(F32), 0.0)
         to_mixed = const.tile([P, P], F32)
         nc.vector.tensor_copy(
             out=to_mixed[:].rearrange("n (e r) -> n e r", e=PACK),
@@ -167,22 +167,22 @@ def tile_modelnew_t_kernel(tc, q, k, v, out):
 
         def mask_v(first):
             codes_by_head = v_codes[:].rearrange("p (h d) -> p h d", d=D)
-            codes_by_slot = masked_v[:].rearrange("p (c s d) -> p c s d", c=LAST, d=D)
+            codes_by_slot = moved_v[:].rearrange("p (c s d) -> p c s d", c=2, d=D)
             scales_by_head = v_scales[:].rearrange("p (h d) -> p h d", d=D)
-            scales_by_slot = moved_scales[:].rearrange("p (c s d) -> p c s d", c=2, d=D)
+            scales_by_slot = chunk_scales[:].rearrange("p (c s d) -> p c s d", c=LAST, d=D)
             slot = first % V_SLOTS
             for c, start, step in ((0, 0, 1), (1, 0, 2), (1, 1, 2), (2, 0, 1)):
                 rows = (c + 1) * QUARTER
                 to = shift_of(start, c) * QUARTER
-                nc.sync.dma_start(
-                    out=codes_by_slot[to : to + rows, c, slot + start : slot + BATCH : step, :].bitcast(I32),
-                    in_=codes_by_head[0:rows, first + start : first + BATCH : step, :].bitcast(I32),
-                )
                 if to > 0:
                     nc.sync.dma_start(
-                        out=scales_by_slot[to : to + rows, c, slot + start : slot + BATCH : step, :].bitcast(I32),
-                        in_=scales_by_head[0:rows, first + start : first + BATCH : step, :].bitcast(I32),
+                        out=codes_by_slot[to : to + rows, c, slot + start : slot + BATCH : step, :].bitcast(I32),
+                        in_=codes_by_head[0:rows, first + start : first + BATCH : step, :].bitcast(I32),
                     )
+                nc.sync.dma_start(
+                    out=scales_by_slot[to : to + rows, c, slot + start : slot + BATCH : step, :].bitcast(I32),
+                    in_=scales_by_head[0:rows, first + start : first + BATCH : step, :].bitcast(I32),
+                )
 
         def permute_mask():
             causal_ps = psum.tile([P, S], F32, tag="past_a")
@@ -335,8 +335,8 @@ def tile_modelnew_t_kernel(tc, q, k, v, out):
                 for c in sorted(range(CHUNKS), key=lambda c: tile_of(h, c)):
                     t_cols = slice(tile_of(h, c) * P, (tile_of(h, c) + 1) * P)
                     slot_cols = slice((c * V_SLOTS + h % V_SLOTS) * D, (c * V_SLOTS + h % V_SLOTS + 1) * D)
-                    rhs = v_codes[:, v_cols] if c == LAST else masked_v[:, slot_cols]
-                    rhs_scale = moved_scales[:, slot_cols] if shift_of(h, c) > 0 else v_scales[:, v_cols]
+                    rhs = moved_v[:, slot_cols] if shift_of(h, c) > 0 else v_codes[:, v_cols]
+                    rhs_scale = v_scales[:, v_cols] if c == LAST else chunk_scales[:, slot_cols]
                     nc.tensor.matmul_mx(
                         out=o_ps[:, c * P : (c + 1) * P],
                         lhsT=codes[:, t_cols].bitcast(FP8X4),

@@ -389,12 +389,12 @@ def tile_modelnew_t_kernel(tc, q, k, v, out):
                 load_v(step + 9, GROUP)
             if step % GROUP == 1 and step + 7 < HEADS:
                 load_q_k(step + 7, GROUP)
+            if 0 <= step + 1 < HEADS:
+                copy_q_k(step + 1)
             if 0 <= step < HEADS:
                 scores(step)
                 mask(step)
                 square(step)
-            if 0 <= step + 1 < HEADS:
-                copy_q_k(step + 1)
             if step == -1:
                 permute_mask()
             if step % 2 == 0:

@@ -11,6 +11,7 @@ U8 = mybir.dt.uint8
 FP8X4 = mybir.dt.float8_e4m3fn_x4
 ACT = mybir.ActivationFunctionType
 ALU = mybir.AluOpType
+AXES = mybir.AxisListType
 
 B, H, S, D = 4, 8, 512, 128
 HEADS = B * H
@@ -23,6 +24,7 @@ TILES = 5
 LAST = CHUNKS - 1
 GROUP = 4
 BATCH = 4
+TERMS = 3
 PAIR_SLOTS = 4
 V_PIECES = 1
 V_SLOTS = 8
@@ -78,13 +80,9 @@ def tile_modelnew_t_kernel(tc, q, k, v, out):
         v_scales = keep.tile([P, HEADS * D], U8, align_bytes=64)
         moved_v = keep.tile([P, 2 * V_SLOTS * D], U32, align_bytes=64)
         chunk_scales = keep.tile([P, LAST * V_SLOTS * D], U8, align_bytes=64)
-        row_sums = []
-        for slot in range(PAIR_SLOTS):
-            z = keep.tile([P, 2 * 2 * CHUNKS], F32, name="z_%d" % slot)
-            nc.vector.memset(z[:], 0.0)
-            row_sums.append(z)
+        row_sums = keep.tile([P, PAIR_SLOTS * 2 * TERMS * CHUNKS], F32)
+        nc.vector.memset(row_sums[:], 0.0)
         nc.vector.memset(v_scales[:].bitcast(I32), 0)
-        nc.vector.memset(chunk_scales[:].bitcast(I32), 0)
 
         ident_bf = const.tile([P, P], BF16)
         make_identity(nc, ident_bf[:])
@@ -101,8 +99,6 @@ def tile_modelnew_t_kernel(tc, q, k, v, out):
             pattern=[[-1, P]],
             channel_multiplier=1,
         )
-        minus_one = const.tile([P, 2, CHUNKS], F32)
-        nc.gpsimd.memset(minus_one[:], -1.0)
         nc.gpsimd.memset(moved_v[:].bitcast(F32), 0.0)
         to_mixed = const.tile([P, P], F32)
         nc.vector.tensor_copy(
@@ -120,6 +116,11 @@ def tile_modelnew_t_kernel(tc, q, k, v, out):
             in_=causal[:].rearrange("n (w j) -> n j w", j=PACK),
         )
         causal_jw = const.tile([P, P], F32)
+        by_term = row_sums[:].rearrange("p (a s c) -> p a s c", s=TERMS, c=CHUNKS)
+        nc.vector.tensor_scalar(
+            out=by_term[:, :, TERMS - 1, :], in0=by_term[:, :, TERMS - 1, :], scalar1=EPS, scalar2=None, op0=ALU.add
+        )
+        nc.vector.memset(chunk_scales[:].bitcast(I32), 0)
 
         q_sb, k_sb, v_sb = {}, {}, {}
 
@@ -140,7 +141,11 @@ def tile_modelnew_t_kernel(tc, q, k, v, out):
 
         turned, transposed, banks, diagonal = {}, {}, {}, {}
         squares, turned_squares, grouped_squares, quantised = {}, {}, {}, {}
-        grouped_values, inverses, products, plain_sums = {}, {}, {}, {}
+        grouped_values, inverses, products, denoms = {}, {}, {}, {}
+
+        def sums_of(pair):
+            first = (pair % PAIR_SLOTS) * 2 * TERMS * CHUNKS
+            return row_sums[:, first : first + 2 * TERMS * CHUNKS]
 
         def group_v(pair):
             grouped_v = work.tile([P, 2, D, PACK], BF16, align_bytes=64, tag="grouped_v", bufs=1)
@@ -240,56 +245,47 @@ def tile_modelnew_t_kernel(tc, q, k, v, out):
             )
             diagonal[h] = masked
 
-        def square(h):
+        def square_block(h, c, on_diagonal):
+            s2 = squares[h // 2][:].rearrange("m (t u x) -> m t u x", t=TILES, u=2)
+            lo, hi = diag_rows(h, c) if on_diagonal else past_rows(h, c)
+            scores_in = diagonal[h][:, c * P : (c + 1) * P] if on_diagonal else banks[h][1][c]
+            z_col = ((h % 2) * TERMS + (1 if on_diagonal else 0)) * CHUNKS + c
+            nc.scalar.activation(
+                out=s2[:, tile_of(h, c), :, 2 * lo : 2 * hi].rearrange("m u (w e) -> m u w e", e=2),
+                in_=scores_in.rearrange("m (u e w) -> m u w e", u=2, e=2),
+                func=ACT.Square,
+                scale=SCALE,
+                accum_out=sums_of(h // 2)[:, z_col : z_col + 1],
+            )
+
+        def square(h, order):
             if h % 2 == 0:
                 s2_new = work.tile([P, TILES * 2 * 2 * P], BF16, tag="s2")
                 squares[h // 2] = s2_new
-            s2 = squares[h // 2][:].rearrange("m (t u x) -> m t u x", t=TILES, u=2)
-            z = row_sums[(h // 2) % PAIR_SLOTS]
-            z0 = (h % 2) * 2 * CHUNKS
-            past = banks[h][1]
-            masked = diagonal[h]
-            for c in (1, 3, 2):
-                lo, hi = past_rows(h, c)
-                nc.scalar.activation(
-                    out=s2[:, tile_of(h, c), :, 2 * lo : 2 * hi].rearrange("m u (w e) -> m u w e", e=2),
-                    in_=past[c].rearrange("m (u e w) -> m u w e", u=2, e=2),
-                    func=ACT.Square,
-                    scale=SCALE,
-                    accum_out=z[:, z0 + c : z0 + c + 1],
-                )
-            for c in range(CHUNKS):
-                lo, hi = diag_rows(h, c)
-                nc.scalar.activation(
-                    out=s2[:, tile_of(h, c), :, 2 * lo : 2 * hi].rearrange("m u (w e) -> m u w e", e=2),
-                    in_=masked[:, c * P : (c + 1) * P].rearrange("m (u e w) -> m u w e", u=2, e=2),
-                    func=ACT.Square,
-                    scale=SCALE,
-                    accum_out=z[:, z0 + CHUNKS + c : z0 + CHUNKS + c + 1],
-                )
+            for c, on_diagonal in order:
+                square_block(h, c, on_diagonal)
 
-        def transpose_squares(g):
+        def transpose_bank(g, bank):
             words = squares[g][:].bitcast(F32)
-            turned_squares[g] = {}
-            for bank in (2, 0, 1):
-                tiles = min(2, TILES - 2 * bank)
-                s2t_ps = psum.tile([P, S], F32, tag="ring", bufs=4)
-                if tiles == 1:
-                    nc.tensor.matmul(
-                        out=s2t_ps[:, 2 * P : 2 * P + 4 * CHUNKS],
-                        lhsT=to_plain[:],
-                        rhs=row_sums[g % PAIR_SLOTS][:],
-                        start=True,
-                        stop=True,
-                    )
-                for n in range(2 * tiles):
-                    plane = 4 * bank + n
-                    nc.tensor.transpose(
-                        s2t_ps[:, n * P : (n + 1) * P], words[:, plane * P : (plane + 1) * P], to_plain[:]
-                    )
-                turned_squares[g][bank] = s2t_ps
-            grouped = work.tile([P, TILES * P * PACK], BF16, align_bytes=64, tag="grouped")
-            grouped_squares[g] = grouped
+            tiles = min(2, TILES - 2 * bank)
+            s2t_ps = psum.tile([P, S], F32, tag="ring", bufs=4)
+            if tiles == 1:
+                nc.tensor.matmul(
+                    out=s2t_ps[:, 2 * P : 2 * P + 2 * TERMS * CHUNKS],
+                    lhsT=to_plain[:],
+                    rhs=sums_of(g),
+                    start=True,
+                    stop=True,
+                )
+            for n in range(2 * tiles):
+                plane = 4 * bank + n
+                nc.tensor.transpose(
+                    s2t_ps[:, n * P : (n + 1) * P], words[:, plane * P : (plane + 1) * P], to_plain[:]
+                )
+            turned_squares[g, bank] = s2t_ps
+            if g not in grouped_squares:
+                grouped = work.tile([P, TILES * P * PACK], BF16, align_bytes=64, tag="grouped")
+                grouped_squares[g] = grouped
 
         def copy_squares(g, bank, copy):
             tiles = min(2, TILES - 2 * bank)
@@ -297,56 +293,57 @@ def tile_modelnew_t_kernel(tc, q, k, v, out):
                 out=grouped_squares[g][:]
                 .bitcast(F32)[:, bank * S : bank * S + tiles * 2 * P]
                 .rearrange("p (t m u) -> p t m u", t=tiles, u=2),
-                in_=turned_squares[g][bank][:, 0 : tiles * 2 * P].rearrange("p (t u m) -> p t m u", t=tiles, u=2),
+                in_=turned_squares[g, bank][:, 0 : tiles * 2 * P].rearrange("p (t u m) -> p t m u", t=tiles, u=2),
             )
 
-        def quantise(g):
-            codes = work.tile([P, TILES * P], U32, align_bytes=64, tag="codes")
-            scales = work.tile([P, TILES * P], U8, align_bytes=64, tag="scales")
-            for lo, hi in ((0, 4), (4, TILES)):
-                nc.vector.quantize_mx(
-                    out=codes[:, lo * P : hi * P].bitcast(FP8X4),
-                    scales=scales[:, lo * P : hi * P],
-                    in_=grouped_squares[g][:, lo * P * PACK : hi * P * PACK],
-                )
-            quantised[g] = (codes, scales)
-
-        def copy_sums(g):
-            sums = work.tile([P, 4 * CHUNKS], F32, tag="sums")
-            nc.vector.tensor_copy(out=sums[:], in_=turned_squares[g][2][:, 2 * P : 2 * P + 4 * CHUNKS])
-            plain_sums[g] = sums
+        def quantise(g, lo, hi):
+            if g not in quantised:
+                codes = work.tile([P, TILES * P], U32, align_bytes=64, tag="codes")
+                scales = work.tile([P, TILES * P], U8, align_bytes=64, tag="scales")
+                quantised[g] = (codes, scales)
+            codes, scales = quantised[g]
+            nc.vector.quantize_mx(
+                out=codes[:, lo * P : hi * P].bitcast(FP8X4),
+                scales=scales[:, lo * P : hi * P],
+                in_=grouped_squares[g][:, lo * P * PACK : hi * P * PACK],
+            )
 
         def denominators(g):
-            z = plain_sums[g][:].rearrange("m (a s c) -> m a s c", a=2, s=2)
-            total = work.tile([P, 2, CHUNKS], F32, tag="total")
-            nc.gpsimd.tensor_tensor(out=total[:], in0=z[:, :, 0, :], in1=z[:, :, 1, :], op=ALU.add)
+            terms = turned_squares[g, 2][:, 2 * P : 2 * P + 2 * TERMS * CHUNKS]
             denom = work.tile([P, 2, CHUNKS], F32, tag="denom")
-            nc.gpsimd.tensor_scalar(out=denom[:], in0=total[:], scalar1=EPS, scalar2=1.0, op0=ALU.add, op1=ALU.mult)
+            nc.vector.tensor_reduce(
+                out=denom[:],
+                in_=terms.rearrange("m (a s c) -> m a c s", a=2, s=TERMS),
+                axis=AXES.X,
+                op=ALU.add,
+            )
+            denoms[g] = denom
+
+        def invert(g):
             inverse = work.tile([P, 2, CHUNKS], F32, tag="inverse", bufs=4)
-            nc.gpsimd.tensor_tensor(out=inverse[:], in0=denom[:], in1=minus_one[:], op=ALU.pow)
+            nc.vector.reciprocal(out=inverse[:], in_=denoms[g][:])
             inverses[g] = inverse
 
-        def weighted_values(g):
-            codes, scales = quantised[g]
-            for parity in range(2):
-                h = 2 * g + parity
-                o_ps = psum.tile([P, S], F32, tag="ring", bufs=4)
-                v_cols = slice(h * D, (h + 1) * D)
-                for c in sorted(range(CHUNKS), key=lambda c: tile_of(h, c)):
-                    t_cols = slice(tile_of(h, c) * P, (tile_of(h, c) + 1) * P)
-                    slot_cols = slice((c * V_SLOTS + h % V_SLOTS) * D, (c * V_SLOTS + h % V_SLOTS + 1) * D)
-                    rhs = moved_v[:, slot_cols] if shift_of(h, c) > 0 else v_codes[:, v_cols]
-                    rhs_scale = v_scales[:, v_cols] if c == LAST else chunk_scales[:, slot_cols]
-                    nc.tensor.matmul_mx(
-                        out=o_ps[:, c * P : (c + 1) * P],
-                        lhsT=codes[:, t_cols].bitcast(FP8X4),
-                        lhsT_scale=scales[:, t_cols],
-                        rhs=rhs.bitcast(FP8X4),
-                        rhs_scale=rhs_scale,
-                        start=True,
-                        stop=True,
-                    )
-                products[h] = o_ps
+        def multiply(h, c):
+            codes, scales = quantised[h // 2]
+            v_cols = slice(h * D, (h + 1) * D)
+            t_cols = slice(tile_of(h, c) * P, (tile_of(h, c) + 1) * P)
+            slot_cols = slice((c * V_SLOTS + h % V_SLOTS) * D, (c * V_SLOTS + h % V_SLOTS + 1) * D)
+            rhs = moved_v[:, slot_cols] if shift_of(h, c) > 0 else v_codes[:, v_cols]
+            rhs_scale = v_scales[:, v_cols] if c == LAST else chunk_scales[:, slot_cols]
+            nc.tensor.matmul_mx(
+                out=products[h][:, c * P : (c + 1) * P],
+                lhsT=codes[:, t_cols].bitcast(FP8X4),
+                lhsT_scale=scales[:, t_cols],
+                rhs=rhs.bitcast(FP8X4),
+                rhs_scale=rhs_scale,
+                start=True,
+                stop=True,
+            )
+
+        def weighted_values(h):
+            for c in sorted(range(CHUNKS), key=lambda c: tile_of(h, c)):
+                multiply(h, c)
 
         def scale_and_store(h, on_vector):
             o_ps = products[h]
@@ -375,6 +372,7 @@ def tile_modelnew_t_kernel(tc, q, k, v, out):
         load_v(0, 4)
         load_q_k(4, 4)
         load_v(4, 4)
+        load_v(8, 4)
 
         def next_v(pair):
             quantise_v(pair)
@@ -383,53 +381,94 @@ def tile_modelnew_t_kernel(tc, q, k, v, out):
             if pair + 1 < PAIRS:
                 group_v(pair + 1)
 
+        past_then_diagonal = ((1, False), (3, False), (2, False), (0, True), (1, True), (2, True), (3, True))
+
         group_v(0)
-        for step in range(-2, HEADS + 4):
+        transpose_q_k(0)
+        copy_q_k(0)
+        permute_mask()
+        for step in range(HEADS - 1):
             if step % GROUP == 3 and step + 9 < HEADS:
                 load_v(step + 9, GROUP)
             if step % GROUP == 1 and step + 7 < HEADS:
                 load_q_k(step + 7, GROUP)
-            if 0 <= step + 1 < HEADS:
+            if step > 0:
                 copy_q_k(step + 1)
-            if 0 <= step < HEADS:
-                scores(step)
-                mask(step)
-                square(step)
-            if step == -1:
-                permute_mask()
+            scores(step)
+            mask(step)
+            square(step, past_then_diagonal)
+            if step == 0:
+                transpose_q_k(1)
+                copy_q_k(1)
             if step % 2 == 0:
                 g = (step - 2) // 2
-                live = 0 <= g < PAIRS
-                if live:
-                    transpose_squares(g)
-                if 0 <= step + 2 < HEADS:
+                if g >= 0:
+                    for bank in (2, 0, 1):
+                        transpose_bank(g, bank)
+                if step + 2 < HEADS:
                     transpose_q_k(step + 2)
-                if live:
+                if g >= 0:
                     copy_squares(g, 0, nc.scalar.copy)
-                if live:
                     copy_squares(g, 2, nc.vector.tensor_copy)
-                    copy_sums(g)
-                if 0 <= g - 1 < PAIRS - 1:
-                    quantise(g - 1)
+                    denominators(g)
+                if g >= 1:
+                    quantise(g - 1, 0, 4)
+                    quantise(g - 1, 4, TILES)
                 if step == 0:
                     next_v(0)
-                if 2 <= (step + 2) // 2 < PAIRS:
-                    next_v((step + 2) // 2)
-                if live:
-                    denominators(g)
+                if g >= 0:
+                    invert(g)
             else:
                 g = (step - 5) // 2
-                live = 0 <= g < PAIRS
-                if live:
-                    weighted_values(g)
-                if 0 <= step + 2 < HEADS:
+                if g >= 0:
+                    for h in (2 * g, 2 * g + 1):
+                        o_ps = psum.tile([P, S], F32, tag="ring", bufs=4)
+                        products[h] = o_ps
+                        weighted_values(h)
+                if step + 2 < HEADS:
                     transpose_q_k(step + 2)
-                if 0 <= (step - 3) // 2 < PAIRS:
+                if step >= 3:
                     copy_squares((step - 3) // 2, 1, nc.scalar.copy)
-                if live:
+                if g >= 0:
                     scale_and_store(2 * g, True)
-                    if g == PAIRS - 2:
-                        quantise(PAIRS - 1)
-                    scale_and_store(2 * g + 1, g < PAIRS - 1)
-                if step == 1:
-                    next_v(1)
+                    scale_and_store(2 * g + 1, True)
+                if (step + 1) // 2 < PAIRS:
+                    next_v((step + 1) // 2)
+
+        last = PAIRS - 1
+        even, odd = HEADS - 2, HEADS - 1
+        scores(odd)
+        mask(odd)
+        square(odd, ((3, False), (3, True), (1, False), (1, True), (0, True), (2, False), (2, True)))
+        for h in (even - 4, even - 3):
+            o_ps = psum.tile([P, S], F32, tag="ring", bufs=4)
+            products[h] = o_ps
+            weighted_values(h)
+        for bank in range(3):
+            transpose_bank(last, bank)
+        copy_squares(last - 1, 1, nc.vector.tensor_copy)
+        scale_and_store(even - 4, True)
+        quantise(last - 1, 0, 4)
+        quantise(last - 1, 4, TILES)
+        for bank in range(3):
+            copy_squares(last, bank, nc.scalar.copy)
+        quantise(last, 0, 2)
+        scale_and_store(even - 3, True)
+        o_ps = psum.tile([P, S], F32, tag="qk_ps")
+        products[even - 2] = o_ps
+        weighted_values(even - 2)
+        o_ps = psum.tile([P, S], F32, tag="diag_ps")
+        products[odd - 2] = o_ps
+        weighted_values(odd - 2)
+        scale_and_store(even - 2, False)
+        denominators(last)
+        quantise(last, 2, 4)
+        invert(last)
+        quantise(last, 4, TILES)
+        scale_and_store(odd - 2, True)
+        for h in (even, odd):
+            o_ps = psum.tile([P, S], F32, tag="ring", bufs=4)
+            products[h] = o_ps
+            weighted_values(h)
+        scale_and_store(even, True)
+        scale_and_store(odd, False)

@@ -416,6 +416,8 @@ def tile_modelnew_t_kernel(tc, q, k, v, out):
                     quantise(g - 1, 4, TILES)
                 if step == 0:
                     next_v(0)
+                if 2 <= (step + 2) // 2 < PAIRS:
+                    next_v((step + 2) // 2)
                 if g >= 0:
                     invert(g)
             else:
@@ -432,8 +434,8 @@ def tile_modelnew_t_kernel(tc, q, k, v, out):
                 if g >= 0:
                     scale_and_store(2 * g, True)
                     scale_and_store(2 * g + 1, True)
-                if (step + 1) // 2 < PAIRS:
-                    next_v((step + 1) // 2)
+                if step == 1:
+                    next_v(1)
 
         last = PAIRS - 1
         even, odd = HEADS - 2, HEADS - 1

@@ -27,6 +27,7 @@ BATCH = 4
 TERMS = 3
 PAIR_SLOTS = 4
 V_PIECES = 1
+WARM_UPS = 3
 V_SLOTS = 8
 EPS = 1e-6
 SCALE = D ** -0.5
@@ -81,46 +82,35 @@ def tile_modelnew_t_kernel(tc, q, k, v, out):
         moved_v = keep.tile([P, 2 * V_SLOTS * D], U32, align_bytes=64)
         chunk_scales = keep.tile([P, LAST * V_SLOTS * D], U8, align_bytes=64)
         row_sums = keep.tile([P, PAIR_SLOTS * 2 * TERMS * CHUNKS], F32)
+        warm = const.tile([P, S], BF16)
+        nc.vector.memset(warm[:], 0.0)
         nc.vector.memset(row_sums[:], 0.0)
         nc.vector.memset(v_scales[:].bitcast(I32), 0)
 
         ident_bf = const.tile([P, P], BF16)
         make_identity(nc, ident_bf[:])
+        causal_jw = const.tile([P, P], F32)
+        nc.gpsimd.memset(causal_jw[:], 1.0)
+        for e in range(PACK):
+            quadrant = causal_jw[e * QUARTER : (e + 1) * QUARTER, :]
+            nc.gpsimd.affine_select(
+                out=quadrant,
+                in_=quadrant,
+                compare_op=ALU.is_ge,
+                fill=0.0,
+                base=e,
+                pattern=[[-1, PACK], [-PACK, QUARTER]],
+                channel_multiplier=PACK,
+            )
         ident_f32 = const.tile([P, P], F32)
         make_identity(nc, ident_f32[:])
-        causal = const.tile([P, P], F32)
-        nc.gpsimd.memset(causal[:], 1.0)
-        nc.gpsimd.affine_select(
-            out=causal[:],
-            in_=causal[:],
-            compare_op=ALU.is_ge,
-            fill=0.0,
-            base=0,
-            pattern=[[-1, P]],
-            channel_multiplier=1,
-        )
-        nc.gpsimd.memset(moved_v[:].bitcast(F32), 0.0)
-        to_mixed = const.tile([P, P], F32)
-        nc.vector.tensor_copy(
-            out=to_mixed[:].rearrange("n (e r) -> n e r", e=PACK),
-            in_=ident_f32[:].rearrange("n (r e) -> n e r", e=PACK),
-        )
         to_plain = const.tile([P, P], F32)
-        nc.vector.tensor_copy(
-            out=to_plain[:].rearrange("m (r e) -> m r e", e=PACK),
-            in_=ident_f32[:].rearrange("m (e r) -> m r e", e=PACK),
-        )
-        causal_plain = const.tile([P, P], F32)
-        nc.vector.tensor_copy(
-            out=causal_plain[:].rearrange("n (j w) -> n j w", j=PACK),
-            in_=causal[:].rearrange("n (w j) -> n j w", j=PACK),
-        )
-        causal_jw = const.tile([P, P], F32)
+        nc.gpsimd.memset(moved_v[:].bitcast(F32), 0.0)
+        nc.gpsimd.memset(chunk_scales[:].bitcast(I32), 0)
         by_term = row_sums[:].rearrange("p (a s c) -> p a s c", s=TERMS, c=CHUNKS)
         nc.vector.tensor_scalar(
             out=by_term[:, :, TERMS - 1, :], in0=by_term[:, :, TERMS - 1, :], scalar1=EPS, scalar2=None, op0=ALU.add
         )
-        nc.vector.memset(chunk_scales[:].bitcast(I32), 0)
 
         q_sb, k_sb, v_sb = {}, {}, {}
 
@@ -141,14 +131,20 @@ def tile_modelnew_t_kernel(tc, q, k, v, out):
 
         turned, transposed, banks, diagonal = {}, {}, {}, {}
         squares, turned_squares, grouped_squares, quantised = {}, {}, {}, {}
-        grouped_values, inverses, products, denoms = {}, {}, {}, {}
+        grouped_values, inverses, products, denoms, scaled = {}, {}, {}, {}, {}
 
         def sums_of(pair):
             first = (pair % PAIR_SLOTS) * 2 * TERMS * CHUNKS
             return row_sums[:, first : first + 2 * TERMS * CHUNKS]
 
+        def make_to_plain():
+            nc.vector.tensor_copy(
+                out=to_plain[:].rearrange("m (r e) -> m r e", e=PACK),
+                in_=ident_f32[:].rearrange("m (e r) -> m r e", e=PACK),
+            )
+
         def group_v(pair):
-            grouped_v = work.tile([P, 2, D, PACK], BF16, align_bytes=64, tag="grouped_v", bufs=1)
+            grouped_v = work.tile([P, 2, D, PACK], BF16, align_bytes=64, tag="grouped_v", bufs=2)
             by_column = v_sb[pair].rearrange("p g (j d) -> p g d j", j=PACK)
             for i in range(2):
                 for d0 in range(0, D, D // V_PIECES):
@@ -170,7 +166,7 @@ def tile_modelnew_t_kernel(tc, q, k, v, out):
                 in_=grouped_values[pair][:].rearrange("p g d j -> p (g d j)"),
             )
 
-        def mask_v(first):
+        def mask_v(first, n):
             codes_by_head = v_codes[:].rearrange("p (h d) -> p h d", d=D)
             codes_by_slot = moved_v[:].rearrange("p (c s d) -> p c s d", c=2, d=D)
             scales_by_head = v_scales[:].rearrange("p (h d) -> p h d", d=D)
@@ -181,58 +177,77 @@ def tile_modelnew_t_kernel(tc, q, k, v, out):
                 to = shift_of(start, c) * QUARTER
                 if to > 0:
                     nc.sync.dma_start(
-                        out=codes_by_slot[to : to + rows, c, slot + start : slot + BATCH : step, :].bitcast(I32),
-                        in_=codes_by_head[0:rows, first + start : first + BATCH : step, :].bitcast(I32),
+                        out=codes_by_slot[to : to + rows, c, slot + start : slot + n : step, :].bitcast(I32),
+                        in_=codes_by_head[0:rows, first + start : first + n : step, :].bitcast(I32),
                     )
                 nc.sync.dma_start(
-                    out=scales_by_slot[to : to + rows, c, slot + start : slot + BATCH : step, :].bitcast(I32),
-                    in_=scales_by_head[0:rows, first + start : first + BATCH : step, :].bitcast(I32),
+                    out=scales_by_slot[to : to + rows, c, slot + start : slot + n : step, :].bitcast(I32),
+                    in_=scales_by_head[0:rows, first + start : first + n : step, :].bitcast(I32),
                 )
 
-        def permute_mask():
-            causal_ps = psum.tile([P, S], F32, tag="past_a")
-            nc.tensor.matmul(out=causal_ps[:, 0:P], lhsT=to_mixed[:], rhs=causal_plain[:], start=True, stop=True)
-            nc.vector.tensor_copy(out=causal_jw[:], in_=causal_ps[:, 0:P])
-
-        def transpose_q_k(h):
-            qk_ps = psum.tile([P, 2 * S], BF16, tag="qk_ps")
-            q_cols = qk_ps[:, 0:S].rearrange("d (c e r) -> d e c r", c=CHUNKS, e=PACK)
+        def turn_q(h, bank):
+            q_cols = bank[:, 0:S].rearrange("d (c e r) -> d e c r", c=CHUNKS, e=PACK)
             for e in range(PACK):
                 nc.tensor.transpose(q_cols[:, e, :, :], q_sb[h][:, e * D : (e + 1) * D], ident_bf[:])
+
+        def turn_k(h, bank):
             for j in range(PACK):
-                nc.tensor.transpose(
-                    qk_ps[:, S + j * P : S + (j + 1) * P], k_sb[h][:, j * D : (j + 1) * D], ident_bf[:]
-                )
+                nc.tensor.transpose(bank[:, S + j * P : S + (j + 1) * P], k_sb[h][:, j * D : (j + 1) * D], ident_bf[:])
+
+        def transpose_q_k(h):
+            if h == 1:
+                qk_ps = psum.tile([P, 2 * S], BF16, tag="ring", bufs=4)
+            else:
+                qk_ps = psum.tile([P, 2 * S], BF16, tag="qk_ps")
+            turn_q(h, qk_ps)
+            turn_k(h, qk_ps)
             turned[h] = qk_ps
+
+        def first_q_k():
+            qk_ps = psum.tile([P, 2 * S], BF16, tag="qk_ps")
+            k_ps = psum.tile([P, 2 * S], BF16, tag="ring", bufs=4)
+            turn_q(0, qk_ps)
+            turn_k(0, k_ps)
+            qk_t = work.tile([P, 2 * S], BF16, tag="qk_t")
+            nc.scalar.copy(out=qk_t[:, 0:S], in_=qk_ps[:, 0:S])
+            nc.vector.tensor_copy(out=qk_t[:, S : 2 * S], in_=k_ps[:, S : 2 * S])
+            transposed[0] = qk_t
+
+        def warm_up():
+            warm_ps = psum.tile([P, S], F32, tag="ring", bufs=4)
+            for i in range(WARM_UPS):
+                nc.tensor.matmul(out=warm_ps[:], lhsT=warm[:, 0:P], rhs=warm[:], start=True, stop=True)
 
         def copy_q_k(h):
             qk_t = work.tile([P, 2 * S], BF16, tag="qk_t")
             nc.vector.tensor_copy(out=qk_t[:], in_=turned[h][:])
             transposed[h] = qk_t
 
-        def scores(h):
+        def scores(h, past_order):
             qk_t = transposed[h]
             k_t = qk_t[:, S : 2 * S].rearrange("d (j p) -> d j p", j=PACK)
             diag_ps = psum.tile([P, S], F32, tag="diag_ps")
             past_a = psum.tile([P, S], F32, tag="past_a")
             past_b = psum.tile([P, 2 * P], F32, tag="past_b")
             past = {1: past_a[:, 0:P], 3: past_a[:, P : 4 * P], 2: past_b[:, 0 : 2 * P]}
-            for c in range(CHUNKS):
-                nc.tensor.matmul(
-                    out=diag_ps[:, c * P : (c + 1) * P].rearrange("m (j w) -> m j w", j=PACK),
-                    lhsT=qk_t[:, c * P : (c + 1) * P],
-                    rhs=k_t[:, :, c * QUARTER : (c + 1) * QUARTER],
-                    start=True,
-                    stop=True,
-                )
-            for c in (1, 3, 2):
-                nc.tensor.matmul(
-                    out=past[c].rearrange("m (j w) -> m j w", j=PACK),
-                    lhsT=qk_t[:, c * P : (c + 1) * P],
-                    rhs=k_t[:, :, 0 : c * QUARTER],
-                    start=True,
-                    stop=True,
-                )
+            for c in past_order:
+                if c is None:
+                    for d in range(CHUNKS):
+                        nc.tensor.matmul(
+                            out=diag_ps[:, d * P : (d + 1) * P].rearrange("m (j w) -> m j w", j=PACK),
+                            lhsT=qk_t[:, d * P : (d + 1) * P],
+                            rhs=k_t[:, :, d * QUARTER : (d + 1) * QUARTER],
+                            start=True,
+                            stop=True,
+                        )
+                else:
+                    nc.tensor.matmul(
+                        out=past[c].rearrange("m (j w) -> m j w", j=PACK),
+                        lhsT=qk_t[:, c * P : (c + 1) * P],
+                        rhs=k_t[:, :, 0 : c * QUARTER],
+                        start=True,
+                        stop=True,
+                    )
             banks[h] = (diag_ps, past)
 
         def mask(h):
@@ -345,10 +360,22 @@ def tile_modelnew_t_kernel(tc, q, k, v, out):
             for c in sorted(range(CHUNKS), key=lambda c: tile_of(h, c)):
                 multiply(h, c)
 
+        def scale_chunk(h, c, o_sb):
+            nc.scalar.activation(
+                out=o_sb[:, c, :],
+                in_=products[h][:, c * P : (c + 1) * P],
+                func=ACT.Copy,
+                scale=inverses[h // 2][:, h % 2, c : c + 1],
+            )
+
+        def store(h, c0, c1):
+            nc.sync.dma_start(out=out_rows[:, h, c0:c1, :], in_=scaled[h][:, c0:c1, :])
+
         def scale_and_store(h, on_vector):
             o_ps = products[h]
             inverse = inverses[h // 2]
             o_sb = work.tile([P, CHUNKS, D], F32, tag="o_sb", bufs=8)
+            scaled[h] = o_sb
             if on_vector:
                 nc.vector.tensor_tensor(
                     out=o_sb[:],
@@ -358,13 +385,8 @@ def tile_modelnew_t_kernel(tc, q, k, v, out):
                 )
             else:
                 for c in range(CHUNKS):
-                    nc.scalar.activation(
-                        out=o_sb[:, c, :],
-                        in_=o_ps[:, c * P : (c + 1) * P],
-                        func=ACT.Copy,
-                        scale=inverse[:, h % 2, c : c + 1],
-                    )
-            nc.sync.dma_start(out=out_rows[:, h, :, :], in_=o_sb[:])
+                    scale_chunk(h, c, o_sb)
+            store(h, 0, CHUNKS)
 
         load_q_k(0, 1)
         load_q_k(1, 1)
@@ -372,34 +394,39 @@ def tile_modelnew_t_kernel(tc, q, k, v, out):
         load_v(0, 4)
         load_q_k(4, 4)
         load_v(4, 4)
-        load_v(8, 4)
 
         def next_v(pair):
             quantise_v(pair)
-            if pair % 2 == 1:
-                mask_v(2 * (pair - 1))
-            if pair + 1 < PAIRS:
-                group_v(pair + 1)
+            if pair < 2:
+                mask_v(2 * pair, 2)
+            elif pair % 2 == 1:
+                mask_v(2 * (pair - 1), BATCH)
+            if pair + 2 < PAIRS:
+                group_v(pair + 2)
+
+        def v_step(pair):
+            return max(2 * pair - 2, min(pair + 2, 4))
 
         past_then_diagonal = ((1, False), (3, False), (2, False), (0, True), (1, True), (2, True), (3, True))
 
+        warm_up()
         group_v(0)
-        transpose_q_k(0)
-        copy_q_k(0)
-        permute_mask()
+        group_v(1)
+        first_q_k()
+        transpose_q_k(1)
         for step in range(HEADS - 1):
+            if step == 1:
+                load_v(8, GROUP)
+            if step % GROUP == 3 and step + 5 < HEADS:
+                load_q_k(step + 5, GROUP)
             if step % GROUP == 3 and step + 9 < HEADS:
                 load_v(step + 9, GROUP)
-            if step % GROUP == 1 and step + 7 < HEADS:
-                load_q_k(step + 7, GROUP)
-            if step > 0:
-                copy_q_k(step + 1)
-            scores(step)
+            copy_q_k(step + 1)
+            scores(step, (1, 3, None, 2))
             mask(step)
             square(step, past_then_diagonal)
-            if step == 0:
-                transpose_q_k(1)
-                copy_q_k(1)
+            if step == 1:
+                make_to_plain()
             if step % 2 == 0:
                 g = (step - 2) // 2
                 if g >= 0:
@@ -407,17 +434,14 @@ def tile_modelnew_t_kernel(tc, q, k, v, out):
                         transpose_bank(g, bank)
                 if step + 2 < HEADS:
                     transpose_q_k(step + 2)
+                if g >= 1:
+                    quantise(g - 1, 0, 4)
                 if g >= 0:
                     copy_squares(g, 0, nc.scalar.copy)
                     copy_squares(g, 2, nc.vector.tensor_copy)
                     denominators(g)
                 if g >= 1:
-                    quantise(g - 1, 0, 4)
                     quantise(g - 1, 4, TILES)
-                if step == 0:
-                    next_v(0)
-                if 2 <= (step + 2) // 2 < PAIRS:
-                    next_v((step + 2) // 2)
                 if g >= 0:
                     invert(g)
             else:
@@ -434,28 +458,29 @@ def tile_modelnew_t_kernel(tc, q, k, v, out):
                 if g >= 0:
                     scale_and_store(2 * g, True)
                     scale_and_store(2 * g + 1, True)
-                if step == 1:
-                    next_v(1)
+            for pair in range(PAIRS):
+                if v_step(pair) == step:
+                    next_v(pair)
 
         last = PAIRS - 1
         even, odd = HEADS - 2, HEADS - 1
-        scores(odd)
+        scores(odd, (3, None, 1, 2))
         mask(odd)
         square(odd, ((3, False), (3, True), (1, False), (1, True), (0, True), (2, False), (2, True)))
         for h in (even - 4, even - 3):
             o_ps = psum.tile([P, S], F32, tag="ring", bufs=4)
             products[h] = o_ps
             weighted_values(h)
-        for bank in range(3):
-            transpose_bank(last, bank)
         copy_squares(last - 1, 1, nc.vector.tensor_copy)
         scale_and_store(even - 4, True)
+        for bank in range(3):
+            transpose_bank(last, bank)
+        scale_and_store(even - 3, True)
         quantise(last - 1, 0, 4)
         quantise(last - 1, 4, TILES)
         for bank in range(3):
             copy_squares(last, bank, nc.scalar.copy)
         quantise(last, 0, 2)
-        scale_and_store(even - 3, True)
         o_ps = psum.tile([P, S], F32, tag="qk_ps")
         products[even - 2] = o_ps
         weighted_values(even - 2)
@@ -472,5 +497,18 @@ def tile_modelnew_t_kernel(tc, q, k, v, out):
             o_ps = psum.tile([P, S], F32, tag="ring", bufs=4)
             products[h] = o_ps
             weighted_values(h)
-        scale_and_store(even, True)
-        scale_and_store(odd, False)
+        half = CHUNKS // 2
+        for h in (even, odd):
+            o_sb = work.tile([P, CHUNKS, D], F32, tag="o_sb", bufs=8)
+            scaled[h] = o_sb
+        for on_scalar, on_vector in ((even, odd), (odd, even)):
+            for c in range(half):
+                scale_chunk(on_scalar, c, scaled[on_scalar])
+            store(on_scalar, 0, half)
+            nc.vector.tensor_tensor(
+                out=scaled[on_vector][:, half:CHUNKS, :],
+                in0=products[on_vector][:, half * P : S].rearrange("m (c d) -> m c d", d=D),
+                in1=inverses[last][:, on_vector % 2, half:CHUNKS].unsqueeze(2).to_broadcast([P, CHUNKS - half, D]),
+                op=ALU.mult,
+            )
+            store(on_vector, half, CHUNKS)

@@ -133,9 +133,14 @@ def tile_modelnew_t_kernel(tc, q, k, v, out):
         squares, turned_squares, grouped_squares, quantised = {}, {}, {}, {}
         grouped_values, inverses, products, denoms, scaled = {}, {}, {}, {}, {}
 
-        def sums_of(pair):
+        def sums_of(pair, n):
             first = (pair % PAIR_SLOTS) * 2 * TERMS * CHUNKS
-            return row_sums[:, first : first + 2 * TERMS * CHUNKS]
+            return row_sums[:, first : first + n * 2 * TERMS * CHUNKS]
+
+        def summed_with(g):
+            if g >= PAIRS - 2:
+                return g, 1
+            return g - 1, 2 * (g % 2)
 
         def make_to_plain():
             nc.vector.tensor_copy(
@@ -270,7 +275,7 @@ def tile_modelnew_t_kernel(tc, q, k, v, out):
                 in_=scores_in.rearrange("m (u e w) -> m u w e", u=2, e=2),
                 func=ACT.Square,
                 scale=SCALE,
-                accum_out=sums_of(h // 2)[:, z_col : z_col + 1],
+                accum_out=sums_of(h // 2, 1)[:, z_col : z_col + 1],
             )
 
         def square(h, order):
@@ -284,11 +289,12 @@ def tile_modelnew_t_kernel(tc, q, k, v, out):
             words = squares[g][:].bitcast(F32)
             tiles = min(2, TILES - 2 * bank)
             s2t_ps = psum.tile([P, S], F32, tag="ring", bufs=4)
-            if tiles == 1:
+            first, n = summed_with(g)
+            if tiles == 1 and n > 0:
                 nc.tensor.matmul(
-                    out=s2t_ps[:, 2 * P : 2 * P + 2 * TERMS * CHUNKS],
+                    out=s2t_ps[:, 2 * P : 2 * P + n * 2 * TERMS * CHUNKS],
                     lhsT=to_plain[:],
-                    rhs=sums_of(g),
+                    rhs=sums_of(first, n),
                     start=True,
                     stop=True,
                 )
@@ -324,20 +330,25 @@ def tile_modelnew_t_kernel(tc, q, k, v, out):
             )
 
         def denominators(g):
-            terms = turned_squares[g, 2][:, 2 * P : 2 * P + 2 * TERMS * CHUNKS]
-            denom = work.tile([P, 2, CHUNKS], F32, tag="denom")
-            nc.vector.tensor_reduce(
-                out=denom[:],
-                in_=terms.rearrange("m (a s c) -> m a c s", a=2, s=TERMS),
-                axis=AXES.X,
-                op=ALU.add,
-            )
-            denoms[g] = denom
+            first, n = summed_with(g)
+            if n > 0:
+                terms = turned_squares[g, 2][:, 2 * P : 2 * P + n * 2 * TERMS * CHUNKS]
+                denom = work.tile([P, 2 * 2, CHUNKS], F32, tag="denom")
+                nc.vector.tensor_reduce(
+                    out=denom[:, 0 : 2 * n, :],
+                    in_=terms.rearrange("m (a s c) -> m a c s", s=TERMS, c=CHUNKS),
+                    axis=AXES.X,
+                    op=ALU.add,
+                )
+                denoms[g] = denom
 
         def invert(g):
-            inverse = work.tile([P, 2, CHUNKS], F32, tag="inverse", bufs=4)
-            nc.vector.reciprocal(out=inverse[:], in_=denoms[g][:])
-            inverses[g] = inverse
+            first, n = summed_with(g)
+            if n > 0:
+                inverse = work.tile([P, 2 * 2, CHUNKS], F32, tag="inverse", bufs=4)
+                nc.vector.reciprocal(out=inverse[:, 0 : 2 * n, :], in_=denoms[g][:, 0 : 2 * n, :])
+                for i in range(2 * n):
+                    inverses[2 * first + i] = inverse[:, i, :]
 
         def multiply(h, c):
             codes, scales = quantised[h // 2]
@@ -365,7 +376,7 @@ def tile_modelnew_t_kernel(tc, q, k, v, out):
                 out=o_sb[:, c, :],
                 in_=products[h][:, c * P : (c + 1) * P],
                 func=ACT.Copy,
-                scale=inverses[h // 2][:, h % 2, c : c + 1],
+                scale=inverses[h][:, c : c + 1],
             )
 
         def store(h, c0, c1):
@@ -373,14 +384,13 @@ def tile_modelnew_t_kernel(tc, q, k, v, out):
 
         def scale_and_store(h, on_vector):
             o_ps = products[h]
-            inverse = inverses[h // 2]
             o_sb = work.tile([P, CHUNKS, D], F32, tag="o_sb", bufs=8)
             scaled[h] = o_sb
             if on_vector:
                 nc.vector.tensor_tensor(
                     out=o_sb[:],
                     in0=o_ps[:].rearrange("m (c d) -> m c d", c=CHUNKS),
-                    in1=inverse[:, h % 2, :].unsqueeze(2).to_broadcast([P, CHUNKS, D]),
+                    in1=inverses[h].unsqueeze(2).to_broadcast([P, CHUNKS, D]),
                     op=ALU.mult,
                 )
             else:
@@ -438,7 +448,7 @@ def tile_modelnew_t_kernel(tc, q, k, v, out):
                     quantise(g - 1, 0, 4)
                 if g >= 0:
                     copy_squares(g, 0, nc.scalar.copy)
-                    copy_squares(g, 2, nc.vector.tensor_copy)
+                    copy_squares(g, 2, nc.scalar.copy)
                     denominators(g)
                 if g >= 1:
                     quantise(g - 1, 4, TILES)
@@ -508,7 +518,7 @@ def tile_modelnew_t_kernel(tc, q, k, v, out):
             nc.vector.tensor_tensor(
                 out=scaled[on_vector][:, half:CHUNKS, :],
                 in0=products[on_vector][:, half * P : S].rearrange("m (c d) -> m c d", d=D),
-                in1=inverses[last][:, on_vector % 2, half:CHUNKS].unsqueeze(2).to_broadcast([P, CHUNKS - half, D]),
+                in1=inverses[on_vector][:, half:CHUNKS].unsqueeze(2).to_broadcast([P, CHUNKS - half, D]),
                 op=ALU.mult,
             )
             store(on_vector, half, CHUNKS)

@@ -427,8 +427,10 @@ def tile_modelnew_t_kernel(tc, q, k, v, out):
         for step in range(HEADS - 1):
             if step == 1:
                 load_v(8, GROUP)
-            if step % GROUP == 3 and step + 5 < HEADS:
-                load_q_k(step + 5, GROUP)
+            if step == 3:
+                load_q_k(8, GROUP)
+            if step > 1 and step % GROUP == 1 and step + 7 < HEADS:
+                load_q_k(step + 7, GROUP)
             if step % GROUP == 3 and step + 9 < HEADS:
                 load_v(step + 9, GROUP)
             copy_q_k(step + 1)
@@ -447,8 +449,11 @@ def tile_modelnew_t_kernel(tc, q, k, v, out):
                 if g >= 1:
                     quantise(g - 1, 0, 4)
                 if g >= 0:
+                    if g % 2 == 0:
+                        copy_squares(g, 2, nc.scalar.copy)
                     copy_squares(g, 0, nc.scalar.copy)
-                    copy_squares(g, 2, nc.scalar.copy)
+                    if g % 2 == 1:
+                        copy_squares(g, 2, nc.vector.tensor_copy)
                     denominators(g)
                 if g >= 1:
                     quantise(g - 1, 4, TILES)

@@ -449,16 +449,15 @@ def tile_modelnew_t_kernel(tc, q, k, v, out):
                 if g >= 1:
                     quantise(g - 1, 0, 4)
                 if g >= 0:
-                    if g % 2 == 0:
+                    with_sums = summed_with(g)[1] > 0
+                    if not with_sums:
                         copy_squares(g, 2, nc.scalar.copy)
                     copy_squares(g, 0, nc.scalar.copy)
-                    if g % 2 == 1:
-                        copy_squares(g, 2, nc.vector.tensor_copy)
                     denominators(g)
+                    if with_sums:
+                        copy_squares(g, 2, nc.vector.tensor_copy)
                 if g >= 1:
                     quantise(g - 1, 4, TILES)
-                if g >= 0:
-                    invert(g)
             else:
                 g = (step - 5) // 2
                 if g >= 0:
@@ -476,6 +475,8 @@ def tile_modelnew_t_kernel(tc, q, k, v, out):
             for pair in range(PAIRS):
                 if v_step(pair) == step:
                     next_v(pair)
+            if step % 2 == 0 and step >= 2:
+                invert((step - 2) // 2)
 
         last = PAIRS - 1
         even, odd = HEADS - 2, HEADS - 1
@@ -490,9 +491,10 @@ def tile_modelnew_t_kernel(tc, q, k, v, out):
         scale_and_store(even - 4, True)
         for bank in range(3):
             transpose_bank(last, bank)
-        scale_and_store(even - 3, True)
         quantise(last - 1, 0, 4)
         quantise(last - 1, 4, TILES)
+        scale_and_store(even - 3, True)
+        denominators(last)
         for bank in range(3):
             copy_squares(last, bank, nc.scalar.copy)
         quantise(last, 0, 2)
@@ -503,7 +505,6 @@ def tile_modelnew_t_kernel(tc, q, k, v, out):
         products[odd - 2] = o_ps
         weighted_values(odd - 2)
         scale_and_store(even - 2, False)
-        denominators(last)
         quantise(last, 2, 4)
         invert(last)
         quantise(last, 4, TILES)
@@ -512,18 +513,11 @@ def tile_modelnew_t_kernel(tc, q, k, v, out):
             o_ps = psum.tile([P, S], F32, tag="ring", bufs=4)
             products[h] = o_ps
             weighted_values(h)
+        scale_and_store(even, True)
+        o_sb = work.tile([P, CHUNKS, D], F32, tag="o_sb", bufs=8)
+        scaled[odd] = o_sb
         half = CHUNKS // 2
-        for h in (even, odd):
-            o_sb = work.tile([P, CHUNKS, D], F32, tag="o_sb", bufs=8)
-            scaled[h] = o_sb
-        for on_scalar, on_vector in ((even, odd), (odd, even)):
-            for c in range(half):
-                scale_chunk(on_scalar, c, scaled[on_scalar])
-            store(on_scalar, 0, half)
-            nc.vector.tensor_tensor(
-                out=scaled[on_vector][:, half:CHUNKS, :],
-                in0=products[on_vector][:, half * P : S].rearrange("m (c d) -> m c d", d=D),
-                in1=inverses[on_vector][:, half:CHUNKS].unsqueeze(2).to_broadcast([P, CHUNKS - half, D]),
-                op=ALU.mult,
-            )
-            store(on_vector, half, CHUNKS)
+        for c0 in (0, half):
+            for c in range(c0, c0 + half):
+                scale_chunk(odd, c, o_sb)
+            store(odd, c0, c0 + half)

@@ -407,15 +407,12 @@ def tile_modelnew_t_kernel(tc, q, k, v, out):
 
         def next_v(pair):
             quantise_v(pair)
-            if pair < 2:
-                mask_v(2 * pair, 2)
-            elif pair % 2 == 1:
-                mask_v(2 * (pair - 1), BATCH)
+            mask_v(2 * pair, 2)
             if pair + 2 < PAIRS:
                 group_v(pair + 2)
 
         def v_step(pair):
-            return max(2 * pair - 2, min(pair + 2, 4))
+            return 2 * pair + 2 if pair < 4 else 2 * pair
 
         past_then_diagonal = ((1, False), (3, False), (2, False), (0, True), (1, True), (2, True), (3, True))
 
@@ -450,11 +447,14 @@ def tile_modelnew_t_kernel(tc, q, k, v, out):
                     quantise(g - 1, 0, 4)
                 if g >= 0:
                     with_sums = summed_with(g)[1] > 0
+                    on_vector = with_sums and not (g % 4 == 1 and g < PAIRS - 2)
                     if not with_sums:
                         copy_squares(g, 2, nc.scalar.copy)
                     copy_squares(g, 0, nc.scalar.copy)
                     denominators(g)
-                    if with_sums:
+                    if with_sums and not on_vector:
+                        copy_squares(g, 2, nc.scalar.copy)
+                    if on_vector:
                         copy_squares(g, 2, nc.vector.tensor_copy)
                 if g >= 1:
                     quantise(g - 1, 4, TILES)

from contextlib import ExitStack

import concourse.mybir as mybir
from concourse.masks import make_identity

F32 = mybir.dt.float32
BF16 = mybir.dt.bfloat16
U32 = mybir.dt.uint32
I32 = mybir.dt.int32
U8 = mybir.dt.uint8
FP8X4 = mybir.dt.float8_e4m3fn_x4
ACT = mybir.ActivationFunctionType
ALU = mybir.AluOpType
AXES = mybir.AxisListType

B, H, S, D = 4, 8, 512, 128
HEADS = B * H
PAIRS = HEADS // 2
P = 128
CHUNKS = 4
PACK = 4
QUARTER = P // PACK
TILES = 5
LAST = CHUNKS - 1
GROUP = 4
BATCH = 4
TERMS = 3
PAIR_SLOTS = 4
V_PIECES = 1
WARM_UPS = 3
V_SLOTS = 8
EPS = 1e-6
SCALE = D ** -0.5

FLOPS = 2 * (2 * HEADS * S * S * D)


def shift_of(h, c):
    if c == 0:
        return LAST
    if c == 1 and h % 2 == 1:
        return 2
    return 0


def diag_rows(h, c):
    first = (shift_of(h, c) + c) * QUARTER
    return first, first + QUARTER


def past_rows(h, c):
    first = shift_of(h, c) * QUARTER
    return first, first + c * QUARTER


def tile_of(h, c):
    if c == LAST:
        return h % 2
    if c == 1:
        return 3
    return 2 if (c == 2) == (h % 2 == 0) else 4


def tile_modelnew_t_kernel(tc, q, k, v, out):
    nc = tc.nc
    q_rows = q.rearrange("b h (p e) d -> p (b h) (e d)", e=PACK)
    k_rows = k.rearrange("b h (p j) d -> p (b h) (j d)", j=PACK)
    v_rows = v.rearrange("b h (p j) d -> p (b h) (j d)", j=PACK)
    out_rows = out.rearrange("b h (c m) d -> m (b h) c d", m=P)

    with ExitStack() as ctx:
        const = ctx.enter_context(tc.tile_pool(name="const", bufs=1))
        loads = ctx.enter_context(tc.tile_pool(name="loads", bufs=1))
        keep = ctx.enter_context(tc.tile_pool(name="keep", bufs=1))
        work = ctx.enter_context(tc.tile_pool(name="work", bufs=3))
        psum = ctx.enter_context(tc.psum_pool(name="psum", bufs=1))

        ctx.enter_context(tc.manual_schedule())

        v_codes = keep.tile([P, HEADS * D], U32, align_bytes=64)
        v_scales = keep.tile([P, HEADS * D], U8, align_bytes=64)
        moved_v = keep.tile([P, 2 * V_SLOTS * D], U32, align_bytes=64)
        chunk_scales = keep.tile([P, LAST * V_SLOTS * D], U8, align_bytes=64)
        row_sums = keep.tile([P, PAIR_SLOTS * 2 * TERMS * CHUNKS], F32)
        warm = const.tile([P, S], BF16)
        nc.vector.memset(warm[:], 0.0)
        nc.vector.memset(row_sums[:], 0.0)
        nc.vector.memset(v_scales[:].bitcast(I32), 0)

        ident_bf = const.tile([P, P], BF16)
        make_identity(nc, ident_bf[:])
        causal_jw = const.tile([P, P], F32)
        nc.gpsimd.memset(causal_jw[:], 1.0)
        for e in range(PACK):
            quadrant = causal_jw[e * QUARTER : (e + 1) * QUARTER, :]
            nc.gpsimd.affine_select(
                out=quadrant,
                in_=quadrant,
                compare_op=ALU.is_ge,
                fill=0.0,
                base=e,
                pattern=[[-1, PACK], [-PACK, QUARTER]],
                channel_multiplier=PACK,
            )
        ident_f32 = const.tile([P, P], F32)
        make_identity(nc, ident_f32[:])
        to_plain = const.tile([P, P], F32)
        nc.gpsimd.memset(moved_v[:].bitcast(F32), 0.0)
        nc.gpsimd.memset(chunk_scales[:].bitcast(I32), 0)
        by_term = row_sums[:].rearrange("p (a s c) -> p a s c", s=TERMS, c=CHUNKS)
        nc.vector.tensor_scalar(
            out=by_term[:, :, TERMS - 1, :], in0=by_term[:, :, TERMS - 1, :], scalar1=EPS, scalar2=None, op0=ALU.add
        )

        q_sb, k_sb, v_sb = {}, {}, {}

        def load_q_k(first, n):
            q_g = loads.tile([P, n, PACK * D], BF16, name="q_g%d" % first)
            nc.sync.dma_start(out=q_g[:], in_=q_rows[:, first : first + n, :])
            k_g = loads.tile([P, n, PACK * D], BF16, name="k_g%d" % first)
            nc.sync.dma_start(out=k_g[:], in_=k_rows[:, first : first + n, :])
            for i in range(n):
                q_sb[first + i] = q_g[:, i, :]
                k_sb[first + i] = k_g[:, i, :]

        def load_v(first, n):
            v_g = loads.tile([P, n, PACK * D], BF16, name="v_g%d" % first)
            nc.sync.dma_start(out=v_g[:], in_=v_rows[:, first : first + n, :])
            for i in range(0, n, 2):
                v_sb[(first + i) // 2] = v_g[:, i : i + 2, :]

        turned, transposed, banks, diagonal = {}, {}, {}, {}
        squares, turned_squares, grouped_squares, quantised = {}, {}, {}, {}
        grouped_values, inverses, products, denoms, scaled = {}, {}, {}, {}, {}

        def sums_of(pair, n):
            first = (pair % PAIR_SLOTS) * 2 * TERMS * CHUNKS
            return row_sums[:, first : first + n * 2 * TERMS * CHUNKS]

        def summed_with(g):
            if g >= PAIRS - 2:
                return g, 1
            return g - 1, 2 * (g % 2)

        def make_to_plain():
            nc.vector.tensor_copy(
                out=to_plain[:].rearrange("m (r e) -> m r e", e=PACK),
                in_=ident_f32[:].rearrange("m (e r) -> m r e", e=PACK),
            )

        def group_v(pair):
            grouped_v = work.tile([P, 2, D, PACK], BF16, align_bytes=64, tag="grouped_v", bufs=2)
            by_column = v_sb[pair].rearrange("p g (j d) -> p g d j", j=PACK)
            for i in range(2):
                for d0 in range(0, D, D // V_PIECES):
                    nc.gpsimd.tensor_scalar(
                        out=grouped_v[:, i, d0 : d0 + D // V_PIECES, :],
                        in0=by_column[:, i, d0 : d0 + D // V_PIECES, :],
                        scalar1=1.0,
                        scalar2=0.0,
                        op0=ALU.mult,
                        op1=ALU.add,
                    )
            grouped_values[pair] = grouped_v

        def quantise_v(pair):
            cols = slice(2 * pair * D, (2 * pair + 2) * D)
            nc.vector.quantize_mx(
                out=v_codes[:, cols].bitcast(FP8X4),
                scales=v_scales[:, cols],
                in_=grouped_values[pair][:].rearrange("p g d j -> p (g d j)"),
            )

        def mask_v(first, n):
            codes_by_head = v_codes[:].rearrange("p (h d) -> p h d", d=D)
            codes_by_slot = moved_v[:].rearrange("p (c s d) -> p c s d", c=2, d=D)
            scales_by_head = v_scales[:].rearrange("p (h d) -> p h d", d=D)
            scales_by_slot = chunk_scales[:].rearrange("p (c s d) -> p c s d", c=LAST, d=D)
            slot = first % V_SLOTS
            for c, start, step in ((0, 0, 1), (1, 0, 2), (1, 1, 2), (2, 0, 1)):
                rows = (c + 1) * QUARTER
                to = shift_of(start, c) * QUARTER
                if to > 0:
                    nc.sync.dma_start(
                        out=codes_by_slot[to : to + rows, c, slot + start : slot + n : step, :].bitcast(I32),
                        in_=codes_by_head[0:rows, first + start : first + n : step, :].bitcast(I32),
                    )
                nc.sync.dma_start(
                    out=scales_by_slot[to : to + rows, c, slot + start : slot + n : step, :].bitcast(I32),
                    in_=scales_by_head[0:rows, first + start : first + n : step, :].bitcast(I32),
                )

        def turn_q(h, bank):
            q_cols = bank[:, 0:S].rearrange("d (c e r) -> d e c r", c=CHUNKS, e=PACK)
            for e in range(PACK):
                nc.tensor.transpose(q_cols[:, e, :, :], q_sb[h][:, e * D : (e + 1) * D], ident_bf[:])

        def turn_k(h, bank):
            for j in range(PACK):
                nc.tensor.transpose(bank[:, S + j * P : S + (j + 1) * P], k_sb[h][:, j * D : (j + 1) * D], ident_bf[:])

        def transpose_q_k(h):
            if h == 1:
                qk_ps = psum.tile([P, 2 * S], BF16, tag="ring", bufs=4)
            else:
                qk_ps = psum.tile([P, 2 * S], BF16, tag="qk_ps")
            turn_q(h, qk_ps)
            turn_k(h, qk_ps)
            turned[h] = qk_ps

        def first_q_k():
            qk_ps = psum.tile([P, 2 * S], BF16, tag="qk_ps")
            k_ps = psum.tile([P, 2 * S], BF16, tag="ring", bufs=4)
            turn_q(0, qk_ps)
            turn_k(0, k_ps)
            qk_t = work.tile([P, 2 * S], BF16, tag="qk_t")
            nc.scalar.copy(out=qk_t[:, 0:S], in_=qk_ps[:, 0:S])
            nc.vector.tensor_copy(out=qk_t[:, S : 2 * S], in_=k_ps[:, S : 2 * S])
            transposed[0] = qk_t

        def warm_up():
            warm_ps = psum.tile([P, S], F32, tag="ring", bufs=4)
            for i in range(WARM_UPS):
                nc.tensor.matmul(out=warm_ps[:], lhsT=warm[:, 0:P], rhs=warm[:], start=True, stop=True)

        def copy_q_k(h):
            qk_t = work.tile([P, 2 * S], BF16, tag="qk_t")
            nc.vector.tensor_copy(out=qk_t[:], in_=turned[h][:])
            transposed[h] = qk_t

        def scores(h, past_order):
            qk_t = transposed[h]
            k_t = qk_t[:, S : 2 * S].rearrange("d (j p) -> d j p", j=PACK)
            diag_ps = psum.tile([P, S], F32, tag="diag_ps")
            past_a = psum.tile([P, S], F32, tag="past_a")
            past_b = psum.tile([P, 2 * P], F32, tag="past_b")
            past = {1: past_a[:, 0:P], 3: past_a[:, P : 4 * P], 2: past_b[:, 0 : 2 * P]}
            for c in past_order:
                if c is None:
                    for d in range(CHUNKS):
                        nc.tensor.matmul(
                            out=diag_ps[:, d * P : (d + 1) * P].rearrange("m (j w) -> m j w", j=PACK),
                            lhsT=qk_t[:, d * P : (d + 1) * P],
                            rhs=k_t[:, :, d * QUARTER : (d + 1) * QUARTER],
                            start=True,
                            stop=True,
                        )
                else:
                    nc.tensor.matmul(
                        out=past[c].rearrange("m (j w) -> m j w", j=PACK),
                        lhsT=qk_t[:, c * P : (c + 1) * P],
                        rhs=k_t[:, :, 0 : c * QUARTER],
                        start=True,
                        stop=True,
                    )
            banks[h] = (diag_ps, past)

        def mask(h):
            masked = work.tile([P, S], F32, tag="masked")
            nc.vector.tensor_tensor(
                out=masked[:].rearrange("m (c x) -> m c x", c=CHUNKS),
                in0=banks[h][0][:].rearrange("m (c x) -> m c x", c=CHUNKS),
                in1=causal_jw[:].unsqueeze(1).to_broadcast([P, CHUNKS, P]),
                op=ALU.mult,
            )
            diagonal[h] = masked

        def square_block(h, c, on_diagonal):
            s2 = squares[h // 2][:].rearrange("m (t u x) -> m t u x", t=TILES, u=2)
            lo, hi = diag_rows(h, c) if on_diagonal else past_rows(h, c)
            scores_in = diagonal[h][:, c * P : (c + 1) * P] if on_diagonal else banks[h][1][c]
            z_col = ((h % 2) * TERMS + (1 if on_diagonal else 0)) * CHUNKS + c
            nc.scalar.activation(
                out=s2[:, tile_of(h, c), :, 2 * lo : 2 * hi].rearrange("m u (w e) -> m u w e", e=2),
                in_=scores_in.rearrange("m (u e w) -> m u w e", u=2, e=2),
                func=ACT.Square,
                scale=SCALE,
                accum_out=sums_of(h // 2, 1)[:, z_col : z_col + 1],
            )

        def square(h, order):
            if h % 2 == 0:
                s2_new = work.tile([P, TILES * 2 * 2 * P], BF16, tag="s2")
                squares[h // 2] = s2_new
            for c, on_diagonal in order:
                square_block(h, c, on_diagonal)

        def transpose_bank(g, bank):
            words = squares[g][:].bitcast(F32)
            tiles = min(2, TILES - 2 * bank)
            s2t_ps = psum.tile([P, S], F32, tag="ring", bufs=4)
            first, n = summed_with(g)
            if tiles == 1 and n > 0:
                nc.tensor.matmul(
                    out=s2t_ps[:, 2 * P : 2 * P + n * 2 * TERMS * CHUNKS],
                    lhsT=to_plain[:],
                    rhs=sums_of(first, n),
                    start=True,
                    stop=True,
                )
            for n in range(2 * tiles):
                plane = 4 * bank + n
                nc.tensor.transpose(
                    s2t_ps[:, n * P : (n + 1) * P], words[:, plane * P : (plane + 1) * P], to_plain[:]
                )
            turned_squares[g, bank] = s2t_ps
            if g not in grouped_squares:
                grouped = work.tile([P, TILES * P * PACK], BF16, align_bytes=64, tag="grouped")
                grouped_squares[g] = grouped

        def copy_squares(g, bank, copy):
            tiles = min(2, TILES - 2 * bank)
            copy(
                out=grouped_squares[g][:]
                .bitcast(F32)[:, bank * S : bank * S + tiles * 2 * P]
                .rearrange("p (t m u) -> p t m u", t=tiles, u=2),
                in_=turned_squares[g, bank][:, 0 : tiles * 2 * P].rearrange("p (t u m) -> p t m u", t=tiles, u=2),
            )

        def quantise(g, lo, hi):
            if g not in quantised:
                codes = work.tile([P, TILES * P], U32, align_bytes=64, tag="codes")
                scales = work.tile([P, TILES * P], U8, align_bytes=64, tag="scales")
                quantised[g] = (codes, scales)
            codes, scales = quantised[g]
            nc.vector.quantize_mx(
                out=codes[:, lo * P : hi * P].bitcast(FP8X4),
                scales=scales[:, lo * P : hi * P],
                in_=grouped_squares[g][:, lo * P * PACK : hi * P * PACK],
            )

        def denominators(g):
            first, n = summed_with(g)
            if n > 0:
                terms = turned_squares[g, 2][:, 2 * P : 2 * P + n * 2 * TERMS * CHUNKS]
                denom = work.tile([P, 2 * 2, CHUNKS], F32, tag="denom")
                nc.vector.tensor_reduce(
                    out=denom[:, 0 : 2 * n, :],
                    in_=terms.rearrange("m (a s c) -> m a c s", s=TERMS, c=CHUNKS),
                    axis=AXES.X,
                    op=ALU.add,
                )
                denoms[g] = denom

        def invert(g):
            first, n = summed_with(g)
            if n > 0:
                inverse = work.tile([P, 2 * 2, CHUNKS], F32, tag="inverse", bufs=4)
                nc.vector.reciprocal(out=inverse[:, 0 : 2 * n, :], in_=denoms[g][:, 0 : 2 * n, :])
                for i in range(2 * n):
                    inverses[2 * first + i] = inverse[:, i, :]

        def multiply(h, c):
            codes, scales = quantised[h // 2]
            v_cols = slice(h * D, (h + 1) * D)
            t_cols = slice(tile_of(h, c) * P, (tile_of(h, c) + 1) * P)
            slot_cols = slice((c * V_SLOTS + h % V_SLOTS) * D, (c * V_SLOTS + h % V_SLOTS + 1) * D)
            rhs = moved_v[:, slot_cols] if shift_of(h, c) > 0 else v_codes[:, v_cols]
            rhs_scale = v_scales[:, v_cols] if c == LAST else chunk_scales[:, slot_cols]
            nc.tensor.matmul_mx(
                out=products[h][:, c * P : (c + 1) * P],
                lhsT=codes[:, t_cols].bitcast(FP8X4),
                lhsT_scale=scales[:, t_cols],
                rhs=rhs.bitcast(FP8X4),
                rhs_scale=rhs_scale,
                start=True,
                stop=True,
            )

        def weighted_values(h):
            for c in sorted(range(CHUNKS), key=lambda c: tile_of(h, c)):
                multiply(h, c)

        def scale_chunk(h, c, o_sb):
            nc.scalar.activation(
                out=o_sb[:, c, :],
                in_=products[h][:, c * P : (c + 1) * P],
                func=ACT.Copy,
                scale=inverses[h][:, c : c + 1],
            )

        def store(h, c0, c1):
            nc.sync.dma_start(out=out_rows[:, h, c0:c1, :], in_=scaled[h][:, c0:c1, :])

        def scale_and_store(h, on_vector):
            o_ps = products[h]
            o_sb = work.tile([P, CHUNKS, D], F32, tag="o_sb", bufs=8)
            scaled[h] = o_sb
            if on_vector:
                nc.vector.tensor_tensor(
                    out=o_sb[:],
                    in0=o_ps[:].rearrange("m (c d) -> m c d", c=CHUNKS),
                    in1=inverses[h].unsqueeze(2).to_broadcast([P, CHUNKS, D]),
                    op=ALU.mult,
                )
            else:
                for c in range(CHUNKS):
                    scale_chunk(h, c, o_sb)
            store(h, 0, CHUNKS)

        load_q_k(0, 1)
        load_q_k(1, 1)
        load_q_k(2, 2)
        load_v(0, 4)
        load_q_k(4, 4)
        load_v(4, 4)

        def next_v(pair):
            quantise_v(pair)
            mask_v(2 * pair, 2)
            if pair + 2 < PAIRS:
                group_v(pair + 2)

        def v_step(pair):
            return 2 * pair + 2 if pair < 4 else 2 * pair

        past_then_diagonal = ((1, False), (3, False), (2, False), (0, True), (1, True), (2, True), (3, True))

        warm_up()
        group_v(0)
        group_v(1)
        first_q_k()
        transpose_q_k(1)
        for step in range(HEADS - 1):
            if step == 1:
                load_v(8, GROUP)
            if step == 3:
                load_q_k(8, GROUP)
            if step > 1 and step % GROUP == 1 and step + 7 < HEADS:
                load_q_k(step + 7, GROUP)
            if step % GROUP == 3 and step + 9 < HEADS:
                load_v(step + 9, GROUP)
            copy_q_k(step + 1)
            scores(step, (1, 3, None, 2))
            mask(step)
            square(step, past_then_diagonal)
            if step == 1:
                make_to_plain()
            if step % 2 == 0:
                g = (step - 2) // 2
                if g >= 0:
                    for bank in (2, 0, 1):
                        transpose_bank(g, bank)
                if step + 2 < HEADS:
                    transpose_q_k(step + 2)
                if g >= 1:
                    quantise(g - 1, 0, 4)
                if g >= 0:
                    with_sums = summed_with(g)[1] > 0
                    on_vector = with_sums and not (g % 4 == 1 and g < PAIRS - 2)
                    if not with_sums:
                        copy_squares(g, 2, nc.scalar.copy)
                    copy_squares(g, 0, nc.scalar.copy)
                    denominators(g)
                    if with_sums and not on_vector:
                        copy_squares(g, 2, nc.scalar.copy)
                    if on_vector:
                        copy_squares(g, 2, nc.vector.tensor_copy)
                if g >= 1:
                    quantise(g - 1, 4, TILES)
            else:
                g = (step - 5) // 2
                if g >= 0:
                    for h in (2 * g, 2 * g + 1):
                        o_ps = psum.tile([P, S], F32, tag="ring", bufs=4)
                        products[h] = o_ps
                        weighted_values(h)
                if step + 2 < HEADS:
                    transpose_q_k(step + 2)
                if step >= 3:
                    copy_squares((step - 3) // 2, 1, nc.scalar.copy)
                if g >= 0:
                    scale_and_store(2 * g, True)
                    scale_and_store(2 * g + 1, True)
            for pair in range(PAIRS):
                if v_step(pair) == step:
                    next_v(pair)
            if step % 2 == 0 and step >= 2:
                invert((step - 2) // 2)

        last = PAIRS - 1
        even, odd = HEADS - 2, HEADS - 1
        scores(odd, (3, None, 1, 2))
        mask(odd)
        square(odd, ((3, False), (3, True), (1, False), (1, True), (0, True), (2, False), (2, True)))
        for h in (even - 4, even - 3):
            o_ps = psum.tile([P, S], F32, tag="ring", bufs=4)
            products[h] = o_ps
            weighted_values(h)
        copy_squares(last - 1, 1, nc.vector.tensor_copy)
        scale_and_store(even - 4, True)
        for bank in range(3):
            transpose_bank(last, bank)
        quantise(last - 1, 0, 4)
        quantise(last - 1, 4, TILES)
        scale_and_store(even - 3, True)
        denominators(last)
        for bank in range(3):
            copy_squares(last, bank, nc.scalar.copy)
        quantise(last, 0, 2)
        o_ps = psum.tile([P, S], F32, tag="qk_ps")
        products[even - 2] = o_ps
        weighted_values(even - 2)
        o_ps = psum.tile([P, S], F32, tag="diag_ps")
        products[odd - 2] = o_ps
        weighted_values(odd - 2)
        scale_and_store(even - 2, False)
        quantise(last, 2, 4)
        invert(last)
        quantise(last, 4, TILES)
        scale_and_store(odd - 2, True)
        for h in (even, odd):
            o_ps = psum.tile([P, S], F32, tag="ring", bufs=4)
            products[h] = o_ps
            weighted_values(h)
        scale_and_store(even, True)
        o_sb = work.tile([P, CHUNKS, D], F32, tag="o_sb", bufs=8)
        scaled[odd] = o_sb
        half = CHUNKS // 2
        for c0 in (0, half):
            for c in range(c0, c0 + half):
                scale_chunk(odd, c, o_sb)
            store(odd, c0, c0 + half)
